import numpy as np
import ml_dtypes


def mxq(x, axis, fmt="e4m3"):
    dtype, down = {"e4m3": (ml_dtypes.float8_e4m3fn, 7), "e5m2": (ml_dtypes.float8_e5m2, 14)}[fmt]
    v = np.moveaxis(np.asarray(x, np.float32).astype(ml_dtypes.bfloat16).astype(np.float64), axis, -1)
    blocks = v.reshape(v.shape[:-1] + (-1, 32))
    amax = np.abs(blocks).max(-1, keepdims=True)
    byte = np.maximum(np.where(amax > 0, np.frexp(amax)[1] - 1 + 127, 0) - down, 1)
    scale = np.exp2(byte - 127.0)
    codes = (blocks / scale).astype(np.float32).astype(dtype).astype(np.float64)
    return np.moveaxis((codes * scale).reshape(v.shape), -1, axis)


WIDE = False


def mx_kscale(k):
    if not WIDE:
        return np.ones(k)
    levels = np.array([10, -10, 5, -5, 0])
    a = np.random.permutation(np.resize(levels, k // 512 * 4)).reshape(k // 512, 4)
    idx = np.arange(k)
    return np.exp2(a[idx // 512, idx % 128 // 32])


BF16 = ml_dtypes.bfloat16


def bf(x):
    return np.asarray(x, np.float32).astype(BF16)


def f64(x):
    return np.asarray(x).astype(np.float64)


B, IN, OUT, R, Q, ORD = 16384, 1024, 1024, 8, 256, 3
K = R ** ORD


def setup_inputs():
    s = mx_kscale(K)[np.arange(R) * (K // R + R)]
    z = np.random.standard_normal((ORD, R, B))
    z[ORD - 1] *= s[:, None]
    g = np.random.standard_normal((Q, K)) / np.sqrt(K) / np.repeat(s, K // R)
    return {"z": bf(z), "G2": bf(g)}


def reference(z, G2):
    Z = f64(z)
    kron = Z[0]
    for j in range(1, ORD):
        kron = kron[None] * Z[j].reshape((R,) + (1,) * j + (B,))
    kron = kron.reshape((-1, B))
    return mxq(f64(G2), 1, "e4m3") @ mxq(kron, 0, "e4m3")

@@ -1,0 +1,162 @@
+from contextlib import ExitStack
+
+import concourse.mybir as mybir
+from concourse.masks import make_identity
+
+F32 = mybir.dt.float32
+BF16 = mybir.dt.bfloat16
+U32 = mybir.dt.uint32
+U8 = mybir.dt.uint8
+FP8X4 = mybir.dt.float8_e4m3fn_x4
+MULT = mybir.AluOpType.mult
+
+P = 128
+R = 8
+K = R * R * R
+PACK = 4
+B = 16384
+Q = 256
+Q_TILES = Q // P
+STRIPES = P // R
+STRIPE = B // STRIPES
+BLOCKS = STRIPE // P
+GROUP = 512
+GROUP_BLOCKS = GROUP // P
+HALF = 2 * P
+
+FLOPS = 2 * Q * K * B
+
+
+def tile_fast_tucker_taylor_pa_t_kernel(tc, z, G2, out):
+    nc = tc.nc
+    with ExitStack() as ctx:
+        ctx.enter_context(tc.manual_schedule())
+        consts = ctx.enter_context(tc.tile_pool(name="consts", bufs=1))
+        work = ctx.enter_context(tc.tile_pool(name="work", bufs=3))
+        stores = ctx.enter_context(tc.tile_pool(name="stores", bufs=4))
+        psum = ctx.enter_context(tc.psum_pool(name="psum", bufs=4))
+
+        z_rows = consts.tile([P, 3, STRIPE], BF16)
+        nc.sync.dma_start(out=z_rows[:], in_=z.rearrange("f a (j x) -> (a j) f x", j=STRIPES))
+        g_rows = consts.tile([P, Q_TILES, K], BF16)
+        nc.scalar.dma_start(out=g_rows[:], in_=G2.rearrange("(t q) k -> q t k", q=P))
+
+        ident_bf16 = consts.tile([P, P], BF16)
+        make_identity(nc, ident_bf16[:])
+        ident_f32 = consts.tile([P, P], F32)
+        make_identity(nc, ident_f32[:])
+
+        turned_z = []
+        for f in range(3):
+            zt = psum.tile([P, BLOCKS, P], BF16, tag="turned", name="zt%d" % f)
+            for i in range(BLOCKS):
+                nc.tensor.transpose(zt[:, i, :], z_rows[:, f, i * P : (i + 1) * P], ident_bf16[:])
+            turned_z.append(zt)
+        z0_t = consts.tile([P, BLOCKS, R, STRIPES], BF16)
+        nc.vector.tensor_copy(
+            out=z0_t[:].rearrange("p i (m h e) j -> p i m h (e j)", m=2, h=2),
+            in_=turned_z[0][:].rearrange("p i (h m r) -> p i m h r", h=2, m=2),
+        )
+        z1_t = consts.tile([P, BLOCKS, R, STRIPES], BF16)
+        nc.vector.tensor_copy(
+            out=z1_t[:].rearrange("p i b j -> p i (b j)"), in_=turned_z[1][:]
+        )
+        z2_t = consts.tile([P, BLOCKS, R, STRIPES], F32)
+        nc.scalar.copy(out=z2_t[:].rearrange("p i c j -> p i (c j)"), in_=turned_z[2][:])
+
+        g_words = g_rows[:].bitcast(F32).rearrange("q t (p u) -> q t u p", u=2)
+        g_turned = psum.tile([P, Q_TILES, 2, P], F32, tag="acc")
+        for t in range(Q_TILES):
+            for u in range(2):
+                nc.tensor.transpose(g_turned[:, t, u, :], g_words[:, t, u, :], ident_f32[:])
+        g_grouped = consts.tile([P, Q_TILES, P, PACK], BF16, align_bytes=64)
+        nc.scalar.copy(
+            out=g_grouped[:].bitcast(F32), in_=g_turned[:].rearrange("p t u q -> p t q u")
+        )
+        g_codes = consts.tile([P, Q], U32, align_bytes=64)
+        g_scales = consts.tile([P, Q], U8, align_bytes=64)
+        nc.vector.quantize_mx(
+            out=g_codes[:].bitcast(FP8X4),
+            scales=g_scales[:],
+            in_=g_grouped[:].rearrange("p t q k -> p (t q k)"),
+        )
+
+        out_view = out.rearrange("(t q) n -> q t n", q=P)
+        groups = B // GROUP
+        groups_per_stripe = STRIPE // GROUP
+
+        def outer_products(j):
+            outer = work.tile([P, BLOCKS, R, R], F32, name="outer")
+            nc.vector.tensor_tensor(
+                out=outer[:],
+                in0=z1_t[:, :, :, j].unsqueeze(3).to_broadcast([P, BLOCKS, R, R]),
+                in1=z0_t[:, :, :, j].unsqueeze(2).to_broadcast([P, BLOCKS, R, R]),
+                op=MULT,
+            )
+            return outer
+
+        def build_group(g, outer):
+            j = g // groups_per_stripe
+            first_block = (g % groups_per_stripe) * GROUP_BLOCKS
+            kron_t = work.tile([P, GROUP_BLOCKS, 2, R, R, PACK], BF16, name="kron_t")
+            kron_words = kron_t[:].bitcast(F32).rearrange("p n u c b w -> p n u (c b w)")
+            grouped = work.tile([P, GROUP, PACK], BF16, align_bytes=64, name="grouped")
+            grouped_words = grouped[:].bitcast(F32)
+            for h in range(GROUP // HALF):
+                for blk in range(2 * h, 2 * h + 2):
+                    i = first_block + blk
+                    for c in range(R):
+                        nc.vector.tensor_scalar(
+                            out=kron_t[:, blk, :, c, :, :],
+                            in0=outer[:, i, :, :].rearrange("p b (m r) -> p m b r", m=2),
+                            scalar1=z2_t[:, i, c, j : j + 1],
+                            scalar2=None,
+                            op0=MULT,
+                        )
+                turned = psum.tile([P, 2, HALF], F32, tag="turned", name="turned")
+                for blk in range(2):
+                    for u in range(2):
+                        nc.tensor.transpose(
+                            turned[:, u, blk * P : (blk + 1) * P],
+                            kron_words[:, 2 * h + blk, u, :],
+                            ident_f32[:],
+                        )
+                nc.scalar.copy(
+                    out=grouped_words[:, h * HALF : (h + 1) * HALF, :],
+                    in_=turned[:].rearrange("p u n -> p n u"),
+                )
+            return grouped
+
+        def contract_group(g, grouped):
+            codes = work.tile([P, GROUP], U32, align_bytes=64, name="codes")
+            scales = work.tile([P, GROUP], U8, align_bytes=64, name="scales")
+            nc.vector.quantize_mx(
+                out=codes[:].bitcast(FP8X4),
+                scales=scales[:],
+                in_=grouped[:].rearrange("p n k -> p (n k)"),
+            )
+            stage = stores.tile([P, Q_TILES, GROUP], F32, name="stage")
+            for t in range(Q_TILES):
+                acc = psum.tile([P, GROUP], F32, tag="acc", name="acc")
+                nc.tensor.matmul_mx(
+                    out=acc[:],
+                    lhsT=g_codes[:, t * P : (t + 1) * P].bitcast(FP8X4),
+                    lhsT_scale=g_scales[:, t * P : (t + 1) * P],
+                    rhs=codes[:].bitcast(FP8X4),
+                    rhs_scale=scales[:],
+                    start=True,
+                    stop=True,
+                )
+                nc.scalar.copy(out=stage[:, t, :], in_=acc[:])
+            nc.sync.dma_start(out=out_view[:, :, g * GROUP : (g + 1) * GROUP], in_=stage[:])
+
+        outer = outer_products(0)
+        waiting = None
+        for g in range(groups):
+            grouped = build_group(g, outer)
+            if (g + 1) % groups_per_stripe == 0 and g + 1 < groups:
+                outer = outer_products((g + 1) // groups_per_stripe)
+            if waiting is not None:
+                contract_group(g - 1, waiting)
+            waiting = grouped
+        contract_group(groups - 1, waiting)

@@ -23,6 +23,7 @@ BLOCKS = STRIPE // P
 GROUP = 512
 GROUP_BLOCKS = GROUP // P
 HALF = 2 * P
+PASS_REPEATS = 2
 
 FLOPS = 2 * Q * K * B
 
@@ -138,15 +139,16 @@ def tile_fast_tucker_taylor_pa_t_kernel(tc, z, G2, out):
             stage = stores.tile([P, Q_TILES, GROUP], F32, name="stage")
             for t in range(Q_TILES):
                 acc = psum.tile([P, GROUP], F32, tag="acc", name="acc")
-                nc.tensor.matmul_mx(
-                    out=acc[:],
-                    lhsT=g_codes[:, t * P : (t + 1) * P].bitcast(FP8X4),
-                    lhsT_scale=g_scales[:, t * P : (t + 1) * P],
-                    rhs=codes[:].bitcast(FP8X4),
-                    rhs_scale=scales[:],
-                    start=True,
-                    stop=True,
-                )
+                for repeat in range(PASS_REPEATS):
+                    nc.tensor.matmul_mx(
+                        out=acc[:],
+                        lhsT=g_codes[:, t * P : (t + 1) * P].bitcast(FP8X4),
+                        lhsT_scale=g_scales[:, t * P : (t + 1) * P],
+                        rhs=codes[:].bitcast(FP8X4),
+                        rhs_scale=scales[:],
+                        start=True,
+                        stop=True,
+                    )
                 nc.scalar.copy(out=stage[:, t, :], in_=acc[:])
             nc.sync.dma_start(out=out_view[:, :, g * GROUP : (g + 1) * GROUP], in_=stage[:])
 

@@ -9,6 +9,7 @@ U32 = mybir.dt.uint32
 U8 = mybir.dt.uint8
 FP8X4 = mybir.dt.float8_e4m3fn_x4
 MULT = mybir.AluOpType.mult
+COPY = mybir.ActivationFunctionType.Copy
 
 P = 128
 R = 8
@@ -23,7 +24,7 @@ BLOCKS = STRIPE // P
 GROUP = 512
 GROUP_BLOCKS = GROUP // P
 HALF = 2 * P
-PASS_REPEATS = 2
+VECTOR_ROWS = 7
 
 FLOPS = 2 * Q * K * B
 
@@ -103,10 +104,19 @@ def tile_fast_tucker_taylor_pa_t_kernel(tc, z, G2, out):
             kron_words = kron_t[:].bitcast(F32).rearrange("p n u c b w -> p n u (c b w)")
             grouped = work.tile([P, GROUP, PACK], BF16, align_bytes=64, name="grouped")
             grouped_words = grouped[:].bitcast(F32)
+            for blk in range(GROUP_BLOCKS):
+                i = first_block + blk
+                for c in range(VECTOR_ROWS, R):
+                    nc.scalar.activation(
+                        out=kron_t[:, blk, :, c, :, :],
+                        in_=outer[:, i, :, :].rearrange("p b (m r) -> p m b r", m=2),
+                        func=COPY,
+                        scale=z2_t[:, i, c, j : j + 1],
+                    )
             for h in range(GROUP // HALF):
                 for blk in range(2 * h, 2 * h + 2):
                     i = first_block + blk
-                    for c in range(R):
+                    for c in range(VECTOR_ROWS):
                         nc.vector.tensor_scalar(
                             out=kron_t[:, blk, :, c, :, :],
                             in0=outer[:, i, :, :].rearrange("p b (m r) -> p m b r", m=2),
@@ -139,16 +149,15 @@ def tile_fast_tucker_taylor_pa_t_kernel(tc, z, G2, out):
             stage = stores.tile([P, Q_TILES, GROUP], F32, name="stage")
             for t in range(Q_TILES):
                 acc = psum.tile([P, GROUP], F32, tag="acc", name="acc")
-                for repeat in range(PASS_REPEATS):
-                    nc.tensor.matmul_mx(
-                        out=acc[:],
-                        lhsT=g_codes[:, t * P : (t + 1) * P].bitcast(FP8X4),
-                        lhsT_scale=g_scales[:, t * P : (t + 1) * P],
-                        rhs=codes[:].bitcast(FP8X4),
-                        rhs_scale=scales[:],
-                        start=True,
-                        stop=True,
-                    )
+                nc.tensor.matmul_mx(
+                    out=acc[:],
+                    lhsT=g_codes[:, t * P : (t + 1) * P].bitcast(FP8X4),
+                    lhsT_scale=g_scales[:, t * P : (t + 1) * P],
+                    rhs=codes[:].bitcast(FP8X4),
+                    rhs_scale=scales[:],
+                    start=True,
+                    stop=True,
+                )
                 nc.scalar.copy(out=stage[:, t, :], in_=acc[:])
             nc.sync.dma_start(out=out_view[:, :, g * GROUP : (g + 1) * GROUP], in_=stage[:])
 

@@ -97,30 +97,37 @@ def tile_fast_tucker_taylor_pa_t_kernel(tc, z, G2, out):
             )
             return outer
 
-        def build_group(g, outer):
+        def new_kron_tile():
+            return work.tile([P, GROUP_BLOCKS, 2, R, R, PACK], BF16, name="kron_t")
+
+        def operands(g, blk, c, outer):
             j = g // groups_per_stripe
-            first_block = (g % groups_per_stripe) * GROUP_BLOCKS
-            kron_t = work.tile([P, GROUP_BLOCKS, 2, R, R, PACK], BF16, name="kron_t")
+            i = (g % groups_per_stripe) * GROUP_BLOCKS + blk
+            return (
+                outer[:, i, :, :].rearrange("p b (m r) -> p m b r", m=2),
+                z2_t[:, i, c, j : j + 1],
+            )
+
+        def scalar_products(g, outer, kron_t):
+            for blk in range(GROUP_BLOCKS):
+                for c in range(VECTOR_ROWS, R):
+                    pairs, factor = operands(g, blk, c, outer)
+                    nc.scalar.activation(
+                        out=kron_t[:, blk, :, c, :, :], in_=pairs, func=COPY, scale=factor
+                    )
+
+        def build_group(g, outer, kron_t):
             kron_words = kron_t[:].bitcast(F32).rearrange("p n u c b w -> p n u (c b w)")
             grouped = work.tile([P, GROUP, PACK], BF16, align_bytes=64, name="grouped")
             grouped_words = grouped[:].bitcast(F32)
-            for blk in range(GROUP_BLOCKS):
-                i = first_block + blk
-                for c in range(VECTOR_ROWS, R):
-                    nc.scalar.activation(
-                        out=kron_t[:, blk, :, c, :, :],
-                        in_=outer[:, i, :, :].rearrange("p b (m r) -> p m b r", m=2),
-                        func=COPY,
-                        scale=z2_t[:, i, c, j : j + 1],
-                    )
             for h in range(GROUP // HALF):
                 for blk in range(2 * h, 2 * h + 2):
-                    i = first_block + blk
                     for c in range(VECTOR_ROWS):
+                        pairs, factor = operands(g, blk, c, outer)
                         nc.vector.tensor_scalar(
                             out=kron_t[:, blk, :, c, :, :],
-                            in0=outer[:, i, :, :].rearrange("p b (m r) -> p m b r", m=2),
-                            scalar1=z2_t[:, i, c, j : j + 1],
+                            in0=pairs,
+                            scalar1=factor,
                             scalar2=None,
                             op0=MULT,
                         )
@@ -162,11 +169,16 @@ def tile_fast_tucker_taylor_pa_t_kernel(tc, z, G2, out):
             nc.sync.dma_start(out=out_view[:, :, g * GROUP : (g + 1) * GROUP], in_=stage[:])
 
         outer = outer_products(0)
+        kron_t = new_kron_tile()
+        scalar_products(0, outer, kron_t)
         waiting = None
         for g in range(groups):
-            grouped = build_group(g, outer)
-            if (g + 1) % groups_per_stripe == 0 and g + 1 < groups:
-                outer = outer_products((g + 1) // groups_per_stripe)
+            grouped = build_group(g, outer, kron_t)
+            if g + 1 < groups:
+                if (g + 1) % groups_per_stripe == 0:
+                    outer = outer_products((g + 1) // groups_per_stripe)
+                kron_t = new_kron_tile()
+                scalar_products(g + 1, outer, kron_t)
             if waiting is not None:
                 contract_group(g - 1, waiting)
             waiting = grouped

@@ -20,10 +20,10 @@ Q = 256
 Q_TILES = Q // P
 STRIPES = P // R
 STRIPE = B // STRIPES
-BLOCKS = STRIPE // P
 GROUP = 512
-GROUP_BLOCKS = GROUP // P
-HALF = 2 * P
+HALVES = STRIPE // GROUP
+BLOCKS = GROUP // P
+BANK = 2 * P
 VECTOR_ROWS = 7
 
 FLOPS = 2 * Q * K * B
@@ -38,8 +38,12 @@ def tile_fast_tucker_taylor_pa_t_kernel(tc, z, G2, out):
         stores = ctx.enter_context(tc.tile_pool(name="stores", bufs=4))
         psum = ctx.enter_context(tc.psum_pool(name="psum", bufs=4))
 
-        z_rows = consts.tile([P, 3, STRIPE], BF16)
-        nc.sync.dma_start(out=z_rows[:], in_=z.rearrange("f a (j x) -> (a j) f x", j=STRIPES))
+        z_view = z.rearrange("f a (j x) -> (a j) f x", j=STRIPES)
+        z_rows = []
+        for half in range(HALVES):
+            rows = consts.tile([P, 3, GROUP], BF16, name="z_rows%d" % half)
+            nc.sync.dma_start(out=rows[:], in_=z_view[:, :, half * GROUP : (half + 1) * GROUP])
+            z_rows.append(rows)
         g_rows = consts.tile([P, Q_TILES, K], BF16)
         nc.scalar.dma_start(out=g_rows[:], in_=G2.rearrange("(t q) k -> q t k", q=P))
 
@@ -48,46 +52,51 @@ def tile_fast_tucker_taylor_pa_t_kernel(tc, z, G2, out):
         ident_f32 = consts.tile([P, P], F32)
         make_identity(nc, ident_f32[:])
 
-        turned_z = []
-        for f in range(3):
-            zt = psum.tile([P, BLOCKS, P], BF16, tag="turned", name="zt%d" % f)
-            for i in range(BLOCKS):
-                nc.tensor.transpose(zt[:, i, :], z_rows[:, f, i * P : (i + 1) * P], ident_bf16[:])
-            turned_z.append(zt)
-        z0_t = consts.tile([P, BLOCKS, R, STRIPES], BF16)
-        nc.vector.tensor_copy(
-            out=z0_t[:].rearrange("p i (m h e) j -> p i m h (e j)", m=2, h=2),
-            in_=turned_z[0][:].rearrange("p i (h m r) -> p i m h r", h=2, m=2),
-        )
-        z1_t = consts.tile([P, BLOCKS, R, STRIPES], BF16)
-        nc.vector.tensor_copy(
-            out=z1_t[:].rearrange("p i b j -> p i (b j)"), in_=turned_z[1][:]
-        )
-        z2_t = consts.tile([P, BLOCKS, R, STRIPES], F32)
-        nc.scalar.copy(out=z2_t[:].rearrange("p i c j -> p i (c j)"), in_=turned_z[2][:])
+        def turn_factors(half):
+            turned_z = []
+            for f in range(3):
+                zt = psum.tile([P, BLOCKS, P], BF16, tag="turned", name="zt%d" % f)
+                for i in range(BLOCKS):
+                    nc.tensor.transpose(
+                        zt[:, i, :], z_rows[half][:, f, i * P : (i + 1) * P], ident_bf16[:]
+                    )
+                turned_z.append(zt)
+            z0_t = consts.tile([P, BLOCKS, R, STRIPES], BF16, name="z0_t%d" % half)
+            nc.vector.tensor_copy(
+                out=z0_t[:].rearrange("p i (m h e) j -> p i m h (e j)", m=2, h=2),
+                in_=turned_z[0][:].rearrange("p i (h m r) -> p i m h r", h=2, m=2),
+            )
+            z1_t = consts.tile([P, BLOCKS, R, STRIPES], BF16, name="z1_t%d" % half)
+            nc.vector.tensor_copy(
+                out=z1_t[:].rearrange("p i b j -> p i (b j)"), in_=turned_z[1][:]
+            )
+            z2_t = consts.tile([P, BLOCKS, R, STRIPES], F32, name="z2_t%d" % half)
+            nc.scalar.copy(out=z2_t[:].rearrange("p i c j -> p i (c j)"), in_=turned_z[2][:])
+            return z0_t, z1_t, z2_t
 
-        g_words = g_rows[:].bitcast(F32).rearrange("q t (p u) -> q t u p", u=2)
-        g_turned = psum.tile([P, Q_TILES, 2, P], F32, tag="acc")
-        for t in range(Q_TILES):
-            for u in range(2):
-                nc.tensor.transpose(g_turned[:, t, u, :], g_words[:, t, u, :], ident_f32[:])
-        g_grouped = consts.tile([P, Q_TILES, P, PACK], BF16, align_bytes=64)
-        nc.scalar.copy(
-            out=g_grouped[:].bitcast(F32), in_=g_turned[:].rearrange("p t u q -> p t q u")
-        )
         g_codes = consts.tile([P, Q], U32, align_bytes=64)
         g_scales = consts.tile([P, Q], U8, align_bytes=64)
-        nc.vector.quantize_mx(
-            out=g_codes[:].bitcast(FP8X4),
-            scales=g_scales[:],
-            in_=g_grouped[:].rearrange("p t q k -> p (t q k)"),
-        )
+
+        def quantise_g2():
+            g_words = g_rows[:].bitcast(F32).rearrange("q t (p u) -> q t u p", u=2)
+            g_turned = psum.tile([P, Q_TILES, 2, P], F32, tag="acc")
+            for t in range(Q_TILES):
+                for u in range(2):
+                    nc.tensor.transpose(g_turned[:, t, u, :], g_words[:, t, u, :], ident_f32[:])
+            g_grouped = consts.tile([P, Q_TILES, P, PACK], BF16, align_bytes=64)
+            nc.scalar.copy(
+                out=g_grouped[:].bitcast(F32), in_=g_turned[:].rearrange("p t u q -> p t q u")
+            )
+            nc.vector.quantize_mx(
+                out=g_codes[:].bitcast(FP8X4),
+                scales=g_scales[:],
+                in_=g_grouped[:].rearrange("p t q k -> p (t q k)"),
+            )
 
         out_view = out.rearrange("(t q) n -> q t n", q=P)
-        groups = B // GROUP
-        groups_per_stripe = STRIPE // GROUP
 
-        def outer_products(j):
+        def start_group(j, factors):
+            z0_t, z1_t, z2_t = factors
             outer = work.tile([P, BLOCKS, R, R], F32, name="outer")
             nc.vector.tensor_tensor(
                 out=outer[:],
@@ -95,57 +104,48 @@ def tile_fast_tucker_taylor_pa_t_kernel(tc, z, G2, out):
                 in1=z0_t[:, :, :, j].unsqueeze(2).to_broadcast([P, BLOCKS, R, R]),
                 op=MULT,
             )
-            return outer
-
-        def new_kron_tile():
-            return work.tile([P, GROUP_BLOCKS, 2, R, R, PACK], BF16, name="kron_t")
-
-        def operands(g, blk, c, outer):
-            j = g // groups_per_stripe
-            i = (g % groups_per_stripe) * GROUP_BLOCKS + blk
-            return (
-                outer[:, i, :, :].rearrange("p b (m r) -> p m b r", m=2),
-                z2_t[:, i, c, j : j + 1],
-            )
-
-        def scalar_products(g, outer, kron_t):
-            for blk in range(GROUP_BLOCKS):
+            kron_t = work.tile([P, BLOCKS, 2, R, R, PACK], BF16, name="kron_t")
+            for i in range(BLOCKS):
                 for c in range(VECTOR_ROWS, R):
-                    pairs, factor = operands(g, blk, c, outer)
                     nc.scalar.activation(
-                        out=kron_t[:, blk, :, c, :, :], in_=pairs, func=COPY, scale=factor
+                        out=kron_t[:, i, :, c, :, :],
+                        in_=outer[:, i, :, :].rearrange("p b (m r) -> p m b r", m=2),
+                        func=COPY,
+                        scale=z2_t[:, i, c, j : j + 1],
                     )
+            return outer, kron_t
 
-        def build_group(g, outer, kron_t):
-            kron_words = kron_t[:].bitcast(F32).rearrange("p n u c b w -> p n u (c b w)")
+        def build_group(j, factors, started):
+            z2_t = factors[2]
+            outer, kron_t = started
+            kron_words = kron_t[:].bitcast(F32).rearrange("p i u c b w -> p i u (c b w)")
             grouped = work.tile([P, GROUP, PACK], BF16, align_bytes=64, name="grouped")
             grouped_words = grouped[:].bitcast(F32)
-            for h in range(GROUP // HALF):
-                for blk in range(2 * h, 2 * h + 2):
+            for h in range(GROUP // BANK):
+                for i in range(2 * h, 2 * h + 2):
                     for c in range(VECTOR_ROWS):
-                        pairs, factor = operands(g, blk, c, outer)
                         nc.vector.tensor_scalar(
-                            out=kron_t[:, blk, :, c, :, :],
-                            in0=pairs,
-                            scalar1=factor,
+                            out=kron_t[:, i, :, c, :, :],
+                            in0=outer[:, i, :, :].rearrange("p b (m r) -> p m b r", m=2),
+                            scalar1=z2_t[:, i, c, j : j + 1],
                             scalar2=None,
                             op0=MULT,
                         )
-                turned = psum.tile([P, 2, HALF], F32, tag="turned", name="turned")
-                for blk in range(2):
+                turned = psum.tile([P, 2, BANK], F32, tag="turned", name="turned")
+                for i in range(2):
                     for u in range(2):
                         nc.tensor.transpose(
-                            turned[:, u, blk * P : (blk + 1) * P],
-                            kron_words[:, 2 * h + blk, u, :],
+                            turned[:, u, i * P : (i + 1) * P],
+                            kron_words[:, 2 * h + i, u, :],
                             ident_f32[:],
                         )
                 nc.scalar.copy(
-                    out=grouped_words[:, h * HALF : (h + 1) * HALF, :],
+                    out=grouped_words[:, h * BANK : (h + 1) * BANK, :],
                     in_=turned[:].rearrange("p u n -> p n u"),
                 )
             return grouped
 
-        def contract_group(g, grouped):
+        def finish_group(n0, grouped):
             codes = work.tile([P, GROUP], U32, align_bytes=64, name="codes")
             scales = work.tile([P, GROUP], U8, align_bytes=64, name="scales")
             nc.vector.quantize_mx(
@@ -153,7 +153,6 @@ def tile_fast_tucker_taylor_pa_t_kernel(tc, z, G2, out):
                 scales=scales[:],
                 in_=grouped[:].rearrange("p n k -> p (n k)"),
             )
-            stage = stores.tile([P, Q_TILES, GROUP], F32, name="stage")
             for t in range(Q_TILES):
                 acc = psum.tile([P, GROUP], F32, tag="acc", name="acc")
                 nc.tensor.matmul_mx(
@@ -165,21 +164,24 @@ def tile_fast_tucker_taylor_pa_t_kernel(tc, z, G2, out):
                     start=True,
                     stop=True,
                 )
-                nc.scalar.copy(out=stage[:, t, :], in_=acc[:])
-            nc.sync.dma_start(out=out_view[:, :, g * GROUP : (g + 1) * GROUP], in_=stage[:])
+                stage = stores.tile([P, GROUP], F32, name="stage")
+                nc.scalar.copy(out=stage[:], in_=acc[:])
+                nc.sync.dma_start(out=out_view[:, t, n0 : n0 + GROUP], in_=stage[:])
 
-        outer = outer_products(0)
-        kron_t = new_kron_tile()
-        scalar_products(0, outer, kron_t)
+        order = [(half, j) for half in range(HALVES) for j in range(STRIPES)]
+        factors = {0: turn_factors(0)}
+        started = start_group(order[0][1], factors[0])
         waiting = None
-        for g in range(groups):
-            grouped = build_group(g, outer, kron_t)
-            if g + 1 < groups:
-                if (g + 1) % groups_per_stripe == 0:
-                    outer = outer_products((g + 1) // groups_per_stripe)
-                kron_t = new_kron_tile()
-                scalar_products(g + 1, outer, kron_t)
+        for g, (half, j) in enumerate(order):
+            grouped = build_group(j, factors[half], started)
+            if g == 0:
+                quantise_g2()
+            if g == STRIPES // 2:
+                factors[1] = turn_factors(1)
+            if g + 1 < len(order):
+                next_half, next_j = order[g + 1]
+                started = start_group(next_j, factors[next_half])
             if waiting is not None:
-                contract_group(g - 1, waiting)
-            waiting = grouped
-        contract_group(groups - 1, waiting)
+                finish_group(waiting[0], waiting[1])
+            waiting = (j * STRIPE + half * GROUP, grouped)
+        finish_group(waiting[0], waiting[1])

@@ -24,9 +24,12 @@ GROUP = 512
 HALVES = STRIPE // GROUP
 BLOCKS = GROUP // P
 BANK = 2 * P
-VECTOR_ROWS = 7
 
 FLOPS = 2 * Q * K * B
+
+
+def on_scalar(i, c):
+    return c == R - 1 and i % 2 == 1
 
 
 def tile_fast_tucker_taylor_pa_t_kernel(tc, z, G2, out):
@@ -97,22 +100,26 @@ def tile_fast_tucker_taylor_pa_t_kernel(tc, z, G2, out):
 
         def start_group(j, factors):
             z0_t, z1_t, z2_t = factors
-            outer = work.tile([P, BLOCKS, R, R], F32, name="outer")
-            nc.vector.tensor_tensor(
-                out=outer[:],
-                in0=z1_t[:, :, :, j].unsqueeze(3).to_broadcast([P, BLOCKS, R, R]),
-                in1=z0_t[:, :, :, j].unsqueeze(2).to_broadcast([P, BLOCKS, R, R]),
-                op=MULT,
-            )
+            outer = work.tile([P, BLOCKS, 2, R, PACK], F32, name="outer")
+            for m in range(2):
+                nc.vector.tensor_tensor(
+                    out=outer[:, :, m, :, :],
+                    in0=z1_t[:, :, :, j].unsqueeze(3).to_broadcast([P, BLOCKS, R, PACK]),
+                    in1=z0_t[:, :, m * PACK : (m + 1) * PACK, j]
+                    .unsqueeze(2)
+                    .to_broadcast([P, BLOCKS, R, PACK]),
+                    op=MULT,
+                )
             kron_t = work.tile([P, BLOCKS, 2, R, R, PACK], BF16, name="kron_t")
             for i in range(BLOCKS):
-                for c in range(VECTOR_ROWS, R):
-                    nc.scalar.activation(
-                        out=kron_t[:, i, :, c, :, :],
-                        in_=outer[:, i, :, :].rearrange("p b (m r) -> p m b r", m=2),
-                        func=COPY,
-                        scale=z2_t[:, i, c, j : j + 1],
-                    )
+                for c in range(R):
+                    if on_scalar(i, c):
+                        nc.scalar.activation(
+                            out=kron_t[:, i, :, c, :, :],
+                            in_=outer[:, i, :, :, :],
+                            func=COPY,
+                            scale=z2_t[:, i, c, j : j + 1],
+                        )
             return outer, kron_t
 
         def build_group(j, factors, started):
@@ -123,14 +130,15 @@ def tile_fast_tucker_taylor_pa_t_kernel(tc, z, G2, out):
             grouped_words = grouped[:].bitcast(F32)
             for h in range(GROUP // BANK):
                 for i in range(2 * h, 2 * h + 2):
-                    for c in range(VECTOR_ROWS):
-                        nc.vector.tensor_scalar(
-                            out=kron_t[:, i, :, c, :, :],
-                            in0=outer[:, i, :, :].rearrange("p b (m r) -> p m b r", m=2),
-                            scalar1=z2_t[:, i, c, j : j + 1],
-                            scalar2=None,
-                            op0=MULT,
-                        )
+                    for c in range(R):
+                        if not on_scalar(i, c):
+                            nc.vector.tensor_scalar(
+                                out=kron_t[:, i, :, c, :, :],
+                                in0=outer[:, i, :, :, :],
+                                scalar1=z2_t[:, i, c, j : j + 1],
+                                scalar2=None,
+                                op0=MULT,
+                            )
                 turned = psum.tile([P, 2, BANK], F32, tag="turned", name="turned")
                 for i in range(2):
                     for u in range(2):

@@ -9,7 +9,6 @@ U32 = mybir.dt.uint32
 U8 = mybir.dt.uint8
 FP8X4 = mybir.dt.float8_e4m3fn_x4
 MULT = mybir.AluOpType.mult
-COPY = mybir.ActivationFunctionType.Copy
 
 P = 128
 R = 8
@@ -26,10 +25,6 @@ BLOCKS = GROUP // P
 BANK = 2 * P
 
 FLOPS = 2 * Q * K * B
-
-
-def on_scalar(i, c):
-    return c == R - 1 and i % 2 == 1
 
 
 def tile_fast_tucker_taylor_pa_t_kernel(tc, z, G2, out):
@@ -99,7 +94,7 @@ def tile_fast_tucker_taylor_pa_t_kernel(tc, z, G2, out):
         out_view = out.rearrange("(t q) n -> q t n", q=P)
 
         def start_group(j, factors):
-            z0_t, z1_t, z2_t = factors
+            z0_t, z1_t = factors[0], factors[1]
             outer = work.tile([P, BLOCKS, 2, R, PACK], F32, name="outer")
             for m in range(2):
                 nc.vector.tensor_tensor(
@@ -110,35 +105,25 @@ def tile_fast_tucker_taylor_pa_t_kernel(tc, z, G2, out):
                     .to_broadcast([P, BLOCKS, R, PACK]),
                     op=MULT,
                 )
-            kron_t = work.tile([P, BLOCKS, 2, R, R, PACK], BF16, name="kron_t")
-            for i in range(BLOCKS):
-                for c in range(R):
-                    if on_scalar(i, c):
-                        nc.scalar.activation(
-                            out=kron_t[:, i, :, c, :, :],
-                            in_=outer[:, i, :, :, :],
-                            func=COPY,
-                            scale=z2_t[:, i, c, j : j + 1],
-                        )
-            return outer, kron_t
+            return outer
 
         def build_group(j, factors, started):
             z2_t = factors[2]
-            outer, kron_t = started
+            outer = started
+            kron_t = work.tile([P, BLOCKS, 2, R, R, PACK], BF16, name="kron_t")
             kron_words = kron_t[:].bitcast(F32).rearrange("p i u c b w -> p i u (c b w)")
             grouped = work.tile([P, GROUP, PACK], BF16, align_bytes=64, name="grouped")
             grouped_words = grouped[:].bitcast(F32)
             for h in range(GROUP // BANK):
                 for i in range(2 * h, 2 * h + 2):
                     for c in range(R):
-                        if not on_scalar(i, c):
-                            nc.vector.tensor_scalar(
-                                out=kron_t[:, i, :, c, :, :],
-                                in0=outer[:, i, :, :, :],
-                                scalar1=z2_t[:, i, c, j : j + 1],
-                                scalar2=None,
-                                op0=MULT,
-                            )
+                        nc.vector.tensor_scalar(
+                            out=kron_t[:, i, :, c, :, :],
+                            in0=outer[:, i, :, :, :],
+                            scalar1=z2_t[:, i, c, j : j + 1],
+                            scalar2=None,
+                            op0=MULT,
+                        )
                 turned = psum.tile([P, 2, BANK], F32, tag="turned", name="turned")
                 for i in range(2):
                     for u in range(2):

@@ -9,6 +9,7 @@ U32 = mybir.dt.uint32
 U8 = mybir.dt.uint8
 FP8X4 = mybir.dt.float8_e4m3fn_x4
 MULT = mybir.AluOpType.mult
+COPY = mybir.ActivationFunctionType.Copy
 
 P = 128
 R = 8
@@ -25,6 +26,10 @@ BLOCKS = GROUP // P
 BANK = 2 * P
 
 FLOPS = 2 * Q * K * B
+
+
+def on_scalar(i, c):
+    return c == R - 1 and i % 2 == 1
 
 
 def tile_fast_tucker_taylor_pa_t_kernel(tc, z, G2, out):
@@ -49,6 +54,16 @@ def tile_fast_tucker_taylor_pa_t_kernel(tc, z, G2, out):
         make_identity(nc, ident_bf16[:])
         ident_f32 = consts.tile([P, P], F32)
         make_identity(nc, ident_f32[:])
+        by_stripe = consts.tile([P, P], BF16)
+        nc.vector.tensor_copy(
+            out=by_stripe[:].rearrange("p (j a) -> p j a", a=R),
+            in_=ident_bf16[:].rearrange("p (a j) -> p j a", a=R),
+        )
+        by_stripe_z0 = consts.tile([P, P], BF16)
+        nc.vector.tensor_copy(
+            out=by_stripe_z0[:].rearrange("p (j m h e) -> p j m h e", m=2, h=2, e=2),
+            in_=ident_bf16[:].rearrange("p (h m e j) -> p j m h e", m=2, h=2, e=2),
+        )
 
         def turn_factors(half):
             turned_z = []
@@ -56,20 +71,21 @@ def tile_fast_tucker_taylor_pa_t_kernel(tc, z, G2, out):
                 zt = psum.tile([P, BLOCKS, P], BF16, tag="turned", name="zt%d" % f)
                 for i in range(BLOCKS):
                     nc.tensor.transpose(
-                        zt[:, i, :], z_rows[half][:, f, i * P : (i + 1) * P], ident_bf16[:]
+                        zt[:, i, :],
+                        z_rows[half][:, f, i * P : (i + 1) * P],
+                        by_stripe_z0[:] if f == 0 else by_stripe[:],
                     )
                 turned_z.append(zt)
-            z0_t = consts.tile([P, BLOCKS, R, STRIPES], BF16, name="z0_t%d" % half)
+            z0_t = consts.tile([P, BLOCKS, STRIPES, R], BF16, name="z0_t%d" % half)
             nc.vector.tensor_copy(
-                out=z0_t[:].rearrange("p i (m h e) j -> p i m h (e j)", m=2, h=2),
-                in_=turned_z[0][:].rearrange("p i (h m r) -> p i m h r", h=2, m=2),
+                out=z0_t[:].rearrange("p i j a -> p i (j a)"), in_=turned_z[0][:]
             )
-            z1_t = consts.tile([P, BLOCKS, R, STRIPES], BF16, name="z1_t%d" % half)
+            z1_t = consts.tile([P, BLOCKS, STRIPES, R], BF16, name="z1_t%d" % half)
             nc.vector.tensor_copy(
-                out=z1_t[:].rearrange("p i b j -> p i (b j)"), in_=turned_z[1][:]
+                out=z1_t[:].rearrange("p i j b -> p i (j b)"), in_=turned_z[1][:]
             )
-            z2_t = consts.tile([P, BLOCKS, R, STRIPES], F32, name="z2_t%d" % half)
-            nc.scalar.copy(out=z2_t[:].rearrange("p i c j -> p i (c j)"), in_=turned_z[2][:])
+            z2_t = consts.tile([P, BLOCKS, STRIPES, R], F32, name="z2_t%d" % half)
+            nc.scalar.copy(out=z2_t[:].rearrange("p i j c -> p i (j c)"), in_=turned_z[2][:])
             return z0_t, z1_t, z2_t
 
         g_codes = consts.tile([P, Q], U32, align_bytes=64)
@@ -94,36 +110,46 @@ def tile_fast_tucker_taylor_pa_t_kernel(tc, z, G2, out):
         out_view = out.rearrange("(t q) n -> q t n", q=P)
 
         def start_group(j, factors):
-            z0_t, z1_t = factors[0], factors[1]
+            z0_t, z1_t, z2_t = factors
             outer = work.tile([P, BLOCKS, 2, R, PACK], F32, name="outer")
             for m in range(2):
                 nc.vector.tensor_tensor(
                     out=outer[:, :, m, :, :],
-                    in0=z1_t[:, :, :, j].unsqueeze(3).to_broadcast([P, BLOCKS, R, PACK]),
-                    in1=z0_t[:, :, m * PACK : (m + 1) * PACK, j]
+                    in0=z1_t[:, :, j, :].unsqueeze(3).to_broadcast([P, BLOCKS, R, PACK]),
+                    in1=z0_t[:, :, j, m * PACK : (m + 1) * PACK]
                     .unsqueeze(2)
                     .to_broadcast([P, BLOCKS, R, PACK]),
                     op=MULT,
                 )
-            return outer
+            kron_t = work.tile([P, BLOCKS, 2, R, R, PACK], BF16, name="kron_t")
+            for i in range(BLOCKS):
+                for c in range(R):
+                    if on_scalar(i, c):
+                        nc.scalar.activation(
+                            out=kron_t[:, i, :, c, :, :],
+                            in_=outer[:, i, :, :, :],
+                            func=COPY,
+                            scale=z2_t[:, i, j, c : c + 1],
+                        )
+            return outer, kron_t
 
         def build_group(j, factors, started):
             z2_t = factors[2]
-            outer = started
-            kron_t = work.tile([P, BLOCKS, 2, R, R, PACK], BF16, name="kron_t")
+            outer, kron_t = started
             kron_words = kron_t[:].bitcast(F32).rearrange("p i u c b w -> p i u (c b w)")
             grouped = work.tile([P, GROUP, PACK], BF16, align_bytes=64, name="grouped")
             grouped_words = grouped[:].bitcast(F32)
             for h in range(GROUP // BANK):
                 for i in range(2 * h, 2 * h + 2):
                     for c in range(R):
-                        nc.vector.tensor_scalar(
-                            out=kron_t[:, i, :, c, :, :],
-                            in0=outer[:, i, :, :, :],
-                            scalar1=z2_t[:, i, c, j : j + 1],
-                            scalar2=None,
-                            op0=MULT,
-                        )
+                        if not on_scalar(i, c):
+                            nc.vector.tensor_scalar(
+                                out=kron_t[:, i, :, c, :, :],
+                                in0=outer[:, i, :, :, :],
+                                scalar1=z2_t[:, i, j, c : c + 1],
+                                scalar2=None,
+                                op0=MULT,
+                            )
                 turned = psum.tile([P, 2, BANK], F32, tag="turned", name="turned")
                 for i in range(2):
                     for u in range(2):

@@ -38,7 +38,7 @@ def tile_fast_tucker_taylor_pa_t_kernel(tc, z, G2, out):
         ctx.enter_context(tc.manual_schedule())
         consts = ctx.enter_context(tc.tile_pool(name="consts", bufs=1))
         work = ctx.enter_context(tc.tile_pool(name="work", bufs=3))
-        stores = ctx.enter_context(tc.tile_pool(name="stores", bufs=4))
+        stores = ctx.enter_context(tc.tile_pool(name="stores", bufs=8))
         psum = ctx.enter_context(tc.psum_pool(name="psum", bufs=4))
 
         z_view = z.rearrange("f a (j x) -> (a j) f x", j=STRIPES)
@@ -76,6 +76,9 @@ def tile_fast_tucker_taylor_pa_t_kernel(tc, z, G2, out):
                         by_stripe_z0[:] if f == 0 else by_stripe[:],
                     )
                 turned_z.append(zt)
+            return turned_z
+
+        def keep_factors(half, turned_z):
             z0_t = consts.tile([P, BLOCKS, STRIPES, R], BF16, name="z0_t%d" % half)
             nc.vector.tensor_copy(
                 out=z0_t[:].rearrange("p i j a -> p i (j a)"), in_=turned_z[0][:]
@@ -91,16 +94,19 @@ def tile_fast_tucker_taylor_pa_t_kernel(tc, z, G2, out):
         g_codes = consts.tile([P, Q], U32, align_bytes=64)
         g_scales = consts.tile([P, Q], U8, align_bytes=64)
 
-        def quantise_g2():
+        g_grouped = consts.tile([P, Q_TILES, P, PACK], BF16, align_bytes=64)
+
+        def turn_g2():
             g_words = g_rows[:].bitcast(F32).rearrange("q t (p u) -> q t u p", u=2)
             g_turned = psum.tile([P, Q_TILES, 2, P], F32, tag="acc")
             for t in range(Q_TILES):
                 for u in range(2):
                     nc.tensor.transpose(g_turned[:, t, u, :], g_words[:, t, u, :], ident_f32[:])
-            g_grouped = consts.tile([P, Q_TILES, P, PACK], BF16, align_bytes=64)
             nc.scalar.copy(
                 out=g_grouped[:].bitcast(F32), in_=g_turned[:].rearrange("p t u q -> p t q u")
             )
+
+        def quantise_g2():
             nc.vector.quantize_mx(
                 out=g_codes[:].bitcast(FP8X4),
                 scales=g_scales[:],
@@ -133,13 +139,12 @@ def tile_fast_tucker_taylor_pa_t_kernel(tc, z, G2, out):
                         )
             return outer, kron_t
 
-        def build_group(j, factors, started):
+        def build_half(j, factors, started, grouped, h):
             z2_t = factors[2]
             outer, kron_t = started
             kron_words = kron_t[:].bitcast(F32).rearrange("p i u c b w -> p i u (c b w)")
-            grouped = work.tile([P, GROUP, PACK], BF16, align_bytes=64, name="grouped")
             grouped_words = grouped[:].bitcast(F32)
-            for h in range(GROUP // BANK):
+            for once in range(1):
                 for i in range(2 * h, 2 * h + 2):
                     for c in range(R):
                         if not on_scalar(i, c):
@@ -162,18 +167,24 @@ def tile_fast_tucker_taylor_pa_t_kernel(tc, z, G2, out):
                     out=grouped_words[:, h * BANK : (h + 1) * BANK, :],
                     in_=turned[:].rearrange("p u n -> p n u"),
                 )
+
+        def build_group(j, factors, started):
+            grouped = work.tile([P, GROUP, PACK], BF16, align_bytes=64, name="grouped")
+            for h in range(GROUP // BANK):
+                build_half(j, factors, started, grouped, h)
             return grouped
 
-        def finish_group(n0, grouped):
-            codes = work.tile([P, GROUP], U32, align_bytes=64, name="codes")
-            scales = work.tile([P, GROUP], U8, align_bytes=64, name="scales")
+        def quantise_and_multiply(grouped, first, width):
+            codes = work.tile([P, width], U32, align_bytes=64, name="codes")
+            scales = work.tile([P, width], U8, align_bytes=64, name="scales")
             nc.vector.quantize_mx(
                 out=codes[:].bitcast(FP8X4),
                 scales=scales[:],
-                in_=grouped[:].rearrange("p n k -> p (n k)"),
+                in_=grouped[:, first : first + width, :].rearrange("p n k -> p (n k)"),
             )
+            accs = []
             for t in range(Q_TILES):
-                acc = psum.tile([P, GROUP], F32, tag="acc", name="acc")
+                acc = psum.tile([P, width], F32, tag="acc", name="acc")
                 nc.tensor.matmul_mx(
                     out=acc[:],
                     lhsT=g_codes[:, t * P : (t + 1) * P].bitcast(FP8X4),
@@ -183,24 +194,51 @@ def tile_fast_tucker_taylor_pa_t_kernel(tc, z, G2, out):
                     start=True,
                     stop=True,
                 )
-                stage = stores.tile([P, GROUP], F32, name="stage")
+                accs.append(acc)
+            return accs
+
+        def leave(acc, t, n0, width, on_vector):
+            stage = stores.tile([P, width], F32, name="stage")
+            if on_vector:
+                nc.vector.tensor_copy(out=stage[:], in_=acc[:])
+            else:
                 nc.scalar.copy(out=stage[:], in_=acc[:])
-                nc.sync.dma_start(out=out_view[:, t, n0 : n0 + GROUP], in_=stage[:])
+            nc.sync.dma_start(out=out_view[:, t, n0 : n0 + width], in_=stage[:])
+
+        def finish_group(n0, grouped):
+            accs = quantise_and_multiply(grouped, 0, GROUP)
+            for t in range(Q_TILES):
+                leave(accs[t], t, n0, GROUP, False)
 
         order = [(half, j) for half in range(HALVES) for j in range(STRIPES)]
-        factors = {0: turn_factors(0)}
+        factors = {0: keep_factors(0, turn_factors(0))}
         started = start_group(order[0][1], factors[0])
         waiting = None
-        for g, (half, j) in enumerate(order):
+        for g, (half, j) in enumerate(order[:-1]):
             grouped = build_group(j, factors[half], started)
             if g == 0:
+                turn_g2()
+            if g == 1:
                 quantise_g2()
             if g == STRIPES // 2:
-                factors[1] = turn_factors(1)
+                turned_z = turn_factors(1)
             if g + 1 < len(order):
                 next_half, next_j = order[g + 1]
                 started = start_group(next_j, factors[next_half])
             if waiting is not None:
                 finish_group(waiting[0], waiting[1])
+            if g == STRIPES // 2:
+                factors[1] = keep_factors(1, turned_z)
             waiting = (j * STRIPE + half * GROUP, grouped)
-        finish_group(waiting[0], waiting[1])
+        half, j = order[-1]
+        n_last = j * STRIPE + half * GROUP
+        grouped = build_group(j, factors[half], started)
+        before = quantise_and_multiply(waiting[1], 0, GROUP)
+        first_half = quantise_and_multiply(grouped, 0, BANK)
+        leave(before[0], 0, waiting[0], GROUP, False)
+        second_half = quantise_and_multiply(grouped, BANK, BANK)
+        leave(before[1], 1, waiting[0], GROUP, True)
+        leave(first_half[0], 0, n_last, BANK, False)
+        leave(first_half[1], 1, n_last, BANK, True)
+        leave(second_half[0], 0, n_last + BANK, BANK, False)
+        leave(second_half[1], 1, n_last + BANK, BANK, True)

@@ -37,7 +37,7 @@ def tile_fast_tucker_taylor_pa_t_kernel(tc, z, G2, out):
     with ExitStack() as ctx:
         ctx.enter_context(tc.manual_schedule())
         consts = ctx.enter_context(tc.tile_pool(name="consts", bufs=1))
-        work = ctx.enter_context(tc.tile_pool(name="work", bufs=3))
+        work = ctx.enter_context(tc.tile_pool(name="work", bufs=4))
         stores = ctx.enter_context(tc.tile_pool(name="stores", bufs=8))
         psum = ctx.enter_context(tc.psum_pool(name="psum", bufs=4))
 
@@ -65,35 +65,29 @@ def tile_fast_tucker_taylor_pa_t_kernel(tc, z, G2, out):
             in_=ident_bf16[:].rearrange("p (h m e j) -> p j m h e", m=2, h=2, e=2),
         )
 
-        def turn_factors(half):
-            turned_z = []
-            for f in range(3):
-                zt = psum.tile([P, BLOCKS, P], BF16, tag="turned", name="zt%d" % f)
-                for i in range(BLOCKS):
-                    nc.tensor.transpose(
-                        zt[:, i, :],
-                        z_rows[half][:, f, i * P : (i + 1) * P],
-                        by_stripe_z0[:] if f == 0 else by_stripe[:],
-                    )
-                turned_z.append(zt)
-            return turned_z
+        def turn_factor(half, f, tag):
+            zt = psum.tile([P, BLOCKS, P], BF16, tag=tag, name="zt")
+            for i in range(BLOCKS):
+                nc.tensor.transpose(
+                    zt[:, i, :],
+                    z_rows[half][:, f, i * P : (i + 1) * P],
+                    by_stripe_z0[:] if f == 0 else by_stripe[:],
+                )
+            return zt
 
-        def keep_factors(half, turned_z):
-            z0_t = consts.tile([P, BLOCKS, STRIPES, R], BF16, name="z0_t%d" % half)
-            nc.vector.tensor_copy(
-                out=z0_t[:].rearrange("p i j a -> p i (j a)"), in_=turned_z[0][:]
+        def keep_factor(half, f, zt):
+            kept = consts.tile(
+                [P, BLOCKS, STRIPES, R], F32 if f == 2 else BF16, name="z%d_t%d" % (f, half)
             )
-            z1_t = consts.tile([P, BLOCKS, STRIPES, R], BF16, name="z1_t%d" % half)
-            nc.vector.tensor_copy(
-                out=z1_t[:].rearrange("p i j b -> p i (j b)"), in_=turned_z[1][:]
-            )
-            z2_t = consts.tile([P, BLOCKS, STRIPES, R], F32, name="z2_t%d" % half)
-            nc.scalar.copy(out=z2_t[:].rearrange("p i j c -> p i (j c)"), in_=turned_z[2][:])
-            return z0_t, z1_t, z2_t
+            flat = kept[:].rearrange("p i j a -> p i (j a)")
+            if f == 2:
+                nc.scalar.copy(out=flat, in_=zt[:])
+            else:
+                nc.vector.tensor_copy(out=flat, in_=zt[:])
+            return kept
 
         g_codes = consts.tile([P, Q], U32, align_bytes=64)
         g_scales = consts.tile([P, Q], U8, align_bytes=64)
-
         g_grouped = consts.tile([P, Q_TILES, P, PACK], BF16, align_bytes=64)
 
         def turn_g2():
@@ -114,9 +108,18 @@ def tile_fast_tucker_taylor_pa_t_kernel(tc, z, G2, out):
             )
 
         out_view = out.rearrange("(t q) n -> q t n", q=P)
+        order = [(half, j) for half in range(HALVES) for j in range(STRIPES)]
+        GROUPS = len(order)
+        factors = {}
+        outers = {}
+        krons = {}
+        turned = {}
+        grouped = {}
+        accs = {}
 
-        def start_group(j, factors):
-            z0_t, z1_t, z2_t = factors
+        def pairs(g):
+            half, j = order[g]
+            z0_t, z1_t = factors[half, 0], factors[half, 1]
             outer = work.tile([P, BLOCKS, 2, R, PACK], F32, name="outer")
             for m in range(2):
                 nc.vector.tensor_tensor(
@@ -127,62 +130,60 @@ def tile_fast_tucker_taylor_pa_t_kernel(tc, z, G2, out):
                     .to_broadcast([P, BLOCKS, R, PACK]),
                     op=MULT,
                 )
-            kron_t = work.tile([P, BLOCKS, 2, R, R, PACK], BF16, name="kron_t")
+            outers[g] = outer
+            krons[g] = work.tile([P, BLOCKS, 2, R, R, PACK], BF16, name="kron_t")
+
+        def scalar_products(g):
+            half, j = order[g]
             for i in range(BLOCKS):
                 for c in range(R):
                     if on_scalar(i, c):
                         nc.scalar.activation(
-                            out=kron_t[:, i, :, c, :, :],
-                            in_=outer[:, i, :, :, :],
+                            out=krons[g][:, i, :, c, :, :],
+                            in_=outers[g][:, i, :, :, :],
                             func=COPY,
-                            scale=z2_t[:, i, j, c : c + 1],
+                            scale=factors[half, 2][:, i, j, c : c + 1],
                         )
-            return outer, kron_t
 
-        def build_half(j, factors, started, grouped, h):
-            z2_t = factors[2]
-            outer, kron_t = started
-            kron_words = kron_t[:].bitcast(F32).rearrange("p i u c b w -> p i u (c b w)")
-            grouped_words = grouped[:].bitcast(F32)
-            for once in range(1):
-                for i in range(2 * h, 2 * h + 2):
-                    for c in range(R):
-                        if not on_scalar(i, c):
-                            nc.vector.tensor_scalar(
-                                out=kron_t[:, i, :, c, :, :],
-                                in0=outer[:, i, :, :, :],
-                                scalar1=z2_t[:, i, j, c : c + 1],
-                                scalar2=None,
-                                op0=MULT,
-                            )
-                turned = psum.tile([P, 2, BANK], F32, tag="turned", name="turned")
-                for i in range(2):
-                    for u in range(2):
-                        nc.tensor.transpose(
-                            turned[:, u, i * P : (i + 1) * P],
-                            kron_words[:, 2 * h + i, u, :],
-                            ident_f32[:],
+        def vector_products(g, h):
+            half, j = order[g]
+            for i in range(2 * h, 2 * h + 2):
+                for c in range(R):
+                    if not on_scalar(i, c):
+                        nc.vector.tensor_scalar(
+                            out=krons[g][:, i, :, c, :, :],
+                            in0=outers[g][:, i, :, :, :],
+                            scalar1=factors[half, 2][:, i, j, c : c + 1],
+                            scalar2=None,
+                            op0=MULT,
                         )
-                nc.scalar.copy(
-                    out=grouped_words[:, h * BANK : (h + 1) * BANK, :],
-                    in_=turned[:].rearrange("p u n -> p n u"),
-                )
 
-        def build_group(j, factors, started):
-            grouped = work.tile([P, GROUP, PACK], BF16, align_bytes=64, name="grouped")
-            for h in range(GROUP // BANK):
-                build_half(j, factors, started, grouped, h)
-            return grouped
+        def turn_half(g, h):
+            words = krons[g][:].bitcast(F32).rearrange("p i u c b w -> p i u (c b w)")
+            bank = psum.tile([P, 2, BANK], F32, tag="turned", name="turned")
+            for i in range(2):
+                for u in range(2):
+                    nc.tensor.transpose(
+                        bank[:, u, i * P : (i + 1) * P], words[:, 2 * h + i, u, :], ident_f32[:]
+                    )
+            turned[g, h] = bank
 
-        def quantise_and_multiply(grouped, first, width):
+        def gather_half(g, h):
+            if h == 0:
+                grouped[g] = work.tile([P, GROUP, PACK], BF16, align_bytes=64, name="grouped")
+            nc.scalar.copy(
+                out=grouped[g][:].bitcast(F32)[:, h * BANK : (h + 1) * BANK, :],
+                in_=turned[g, h][:].rearrange("p u n -> p n u"),
+            )
+
+        def quantise_and_multiply(g, first, width):
             codes = work.tile([P, width], U32, align_bytes=64, name="codes")
             scales = work.tile([P, width], U8, align_bytes=64, name="scales")
             nc.vector.quantize_mx(
                 out=codes[:].bitcast(FP8X4),
                 scales=scales[:],
-                in_=grouped[:, first : first + width, :].rearrange("p n k -> p (n k)"),
+                in_=grouped[g][:, first : first + width, :].rearrange("p n k -> p (n k)"),
             )
-            accs = []
             for t in range(Q_TILES):
                 acc = psum.tile([P, width], F32, tag="acc", name="acc")
                 nc.tensor.matmul_mx(
@@ -194,51 +195,57 @@ def tile_fast_tucker_taylor_pa_t_kernel(tc, z, G2, out):
                     start=True,
                     stop=True,
                 )
-                accs.append(acc)
-            return accs
+                accs[g, first, t] = acc
 
-        def leave(acc, t, n0, width, on_vector):
+        def leave(g, first, width, t, on_vector=False):
+            half, j = order[g]
+            n0 = j * STRIPE + half * GROUP + first
             stage = stores.tile([P, width], F32, name="stage")
             if on_vector:
-                nc.vector.tensor_copy(out=stage[:], in_=acc[:])
+                nc.vector.tensor_copy(out=stage[:], in_=accs[g, first, t][:])
             else:
-                nc.scalar.copy(out=stage[:], in_=acc[:])
+                nc.scalar.copy(out=stage[:], in_=accs[g, first, t][:])
             nc.sync.dma_start(out=out_view[:, t, n0 : n0 + width], in_=stage[:])
 
-        def finish_group(n0, grouped):
-            accs = quantise_and_multiply(grouped, 0, GROUP)
-            for t in range(Q_TILES):
-                leave(accs[t], t, n0, GROUP, False)
-
-        order = [(half, j) for half in range(HALVES) for j in range(STRIPES)]
-        factors = {0: keep_factors(0, turn_factors(0))}
-        started = start_group(order[0][1], factors[0])
-        waiting = None
-        for g, (half, j) in enumerate(order[:-1]):
-            grouped = build_group(j, factors[half], started)
+        first_z = [turn_factor(0, f, "turned") for f in range(3)]
+        for f in range(3):
+            factors[0, f] = keep_factor(0, f, first_z[f])
+        pairs(0)
+        scalar_products(0)
+        late_z = {}
+        for g in range(GROUPS):
+            if g == 2:
+                quantise_g2()
+            if g >= 2:
+                quantise_and_multiply(g - 2, 0, GROUP)
+            if g + 1 < GROUPS:
+                pairs(g + 1)
+            for h in range(2):
+                vector_products(g, h)
+                turn_half(g, h)
             if g == 0:
                 turn_g2()
-            if g == 1:
-                quantise_g2()
-            if g == STRIPES // 2:
-                turned_z = turn_factors(1)
-            if g + 1 < len(order):
-                next_half, next_j = order[g + 1]
-                started = start_group(next_j, factors[next_half])
-            if waiting is not None:
-                finish_group(waiting[0], waiting[1])
-            if g == STRIPES // 2:
-                factors[1] = keep_factors(1, turned_z)
-            waiting = (j * STRIPE + half * GROUP, grouped)
-        half, j = order[-1]
-        n_last = j * STRIPE + half * GROUP
-        grouped = build_group(j, factors[half], started)
-        before = quantise_and_multiply(waiting[1], 0, GROUP)
-        first_half = quantise_and_multiply(grouped, 0, BANK)
-        leave(before[0], 0, waiting[0], GROUP, False)
-        second_half = quantise_and_multiply(grouped, BANK, BANK)
-        leave(before[1], 1, waiting[0], GROUP, True)
-        leave(first_half[0], 0, n_last, BANK, False)
-        leave(first_half[1], 1, n_last, BANK, True)
-        leave(second_half[0], 0, n_last + BANK, BANK, False)
-        leave(second_half[1], 1, n_last + BANK, BANK, True)
+            if g >= 1:
+                gather_half(g - 1, 0)
+                gather_half(g - 1, 1)
+            if g + 1 < GROUPS:
+                scalar_products(g + 1)
+            if g >= 2:
+                leave(g - 2, 0, GROUP, 0)
+                leave(g - 2, 0, GROUP, 1)
+            if g in (8, 10, 12):
+                late_z[(g - 8) // 2] = turn_factor(1, (g - 8) // 2, "acc")
+            if g in (9, 11, 13):
+                factors[1, (g - 9) // 2] = keep_factor(1, (g - 9) // 2, late_z[(g - 9) // 2])
+        last = GROUPS - 1
+        gather_half(last, 0)
+        gather_half(last, 1)
+        quantise_and_multiply(last - 1, 0, GROUP)
+        quantise_and_multiply(last, 0, BANK)
+        leave(last - 1, 0, GROUP, 0)
+        quantise_and_multiply(last, BANK, BANK)
+        leave(last - 1, 0, GROUP, 1, True)
+        leave(last, 0, BANK, 0)
+        leave(last, 0, BANK, 1, True)
+        leave(last, BANK, BANK, 0)
+        leave(last, BANK, BANK, 1, True)

@@ -20,16 +20,21 @@ Q = 256
 Q_TILES = Q // P
 STRIPES = P // R
 STRIPE = B // STRIPES
-GROUP = 512
-HALVES = STRIPE // GROUP
-BLOCKS = GROUP // P
+SLICES = STRIPE // P
+BLOCKS = 4
+GROUP = BLOCKS * P
+QUADS = STRIPES // BLOCKS
 BANK = 2 * P
+GROUPS = SLICES * QUADS
+CHUNKS = ((0, 1), (1, 4), (4, 8))
 
 FLOPS = 2 * Q * K * B
 
 
-def on_scalar(i, c):
-    return c == R - 1 and i % 2 == 1
+def on_scalar(g, blk, c):
+    if g == 0:
+        return c >= R - 2
+    return g < GROUPS - 8 and c == R - 1 and blk % 2 == 1
 
 
 def tile_fast_tucker_taylor_pa_t_kernel(tc, z, G2, out):
@@ -41,11 +46,11 @@ def tile_fast_tucker_taylor_pa_t_kernel(tc, z, G2, out):
         stores = ctx.enter_context(tc.tile_pool(name="stores", bufs=8))
         psum = ctx.enter_context(tc.psum_pool(name="psum", bufs=4))
 
-        z_view = z.rearrange("f a (j x) -> (a j) f x", j=STRIPES)
+        z_view = z.rearrange("f a (j i x) -> (a j) f i x", j=STRIPES, x=P)
         z_rows = []
-        for half in range(HALVES):
-            rows = consts.tile([P, 3, GROUP], BF16, name="z_rows%d" % half)
-            nc.sync.dma_start(out=rows[:], in_=z_view[:, :, half * GROUP : (half + 1) * GROUP])
+        for k, (first, end) in enumerate(CHUNKS):
+            rows = consts.tile([P, 3, end - first, P], BF16, name="z_rows%d" % k)
+            nc.sync.dma_start(out=rows[:], in_=z_view[:, :, first:end, :])
             z_rows.append(rows)
         g_rows = consts.tile([P, Q_TILES, K], BF16)
         nc.scalar.dma_start(out=g_rows[:], in_=G2.rearrange("(t q) k -> q t k", q=P))
@@ -65,26 +70,40 @@ def tile_fast_tucker_taylor_pa_t_kernel(tc, z, G2, out):
             in_=ident_bf16[:].rearrange("p (h m e j) -> p j m h e", m=2, h=2, e=2),
         )
 
-        def turn_factor(half, f, tag):
-            zt = psum.tile([P, BLOCKS, P], BF16, tag=tag, name="zt")
-            for i in range(BLOCKS):
-                nc.tensor.transpose(
-                    zt[:, i, :],
-                    z_rows[half][:, f, i * P : (i + 1) * P],
-                    by_stripe_z0[:] if f == 0 else by_stripe[:],
-                )
-            return zt
+        def turn_z(k, tag):
+            slices = CHUNKS[k][1] - CHUNKS[k][0]
+            z01 = psum.tile([P, 2, slices, P], BF16, tag=tag, name="z01")
+            z2 = psum.tile([P, slices, P], BF16, tag=tag, name="z2")
+            for f in range(3):
+                for i in range(slices):
+                    nc.tensor.transpose(
+                        z2[:, i, :] if f == 2 else z01[:, f, i, :],
+                        z_rows[k][:, f, i, :],
+                        by_stripe_z0[:] if f == 0 else by_stripe[:],
+                    )
+            return z01, z2
 
-        def keep_factor(half, f, zt):
-            kept = consts.tile(
-                [P, BLOCKS, STRIPES, R], F32 if f == 2 else BF16, name="z%d_t%d" % (f, half)
+        z01_t = {}
+        z2_t = {}
+
+        def keep_z(k, turned_z, copy_z01):
+            slices = CHUNKS[k][1] - CHUNKS[k][0]
+            z01_t[k] = consts.tile([P, 2, slices, STRIPES, R], BF16, name="z01_t%d" % k)
+            copy_z01(
+                out=z01_t[k][:].rearrange("p f i j a -> p (f i j a)"),
+                in_=turned_z[0][:].rearrange("p f i x -> p (f i x)"),
             )
-            flat = kept[:].rearrange("p i j a -> p i (j a)")
-            if f == 2:
-                nc.scalar.copy(out=flat, in_=zt[:])
-            else:
-                nc.vector.tensor_copy(out=flat, in_=zt[:])
-            return kept
+            z2_t[k] = consts.tile([P, slices, STRIPES, R], F32, name="z2_t%d" % k)
+            nc.scalar.copy(
+                out=z2_t[k][:].rearrange("p i j a -> p (i j a)"),
+                in_=turned_z[1][:].rearrange("p i x -> p (i x)"),
+            )
+
+        def place(g):
+            i = g // QUADS
+            for k, (first, end) in enumerate(CHUNKS):
+                if first <= i < end:
+                    return k, i - first, g % QUADS * BLOCKS
 
         g_codes = consts.tile([P, Q], U32, align_bytes=64)
         g_scales = consts.tile([P, Q], U8, align_bytes=64)
@@ -107,25 +126,24 @@ def tile_fast_tucker_taylor_pa_t_kernel(tc, z, G2, out):
                 in_=g_grouped[:].rearrange("p t q k -> p (t q k)"),
             )
 
-        out_view = out.rearrange("(t q) n -> q t n", q=P)
-        order = [(half, j) for half in range(HALVES) for j in range(STRIPES)]
-        GROUPS = len(order)
-        factors = {}
+        out_view = out.rearrange("(t q) (j i x) -> q t i j x", q=P, j=STRIPES, x=P)
         outers = {}
         krons = {}
         turned = {}
         grouped = {}
+        quantised = {}
         accs = {}
 
         def pairs(g):
-            half, j = order[g]
-            z0_t, z1_t = factors[half, 0], factors[half, 1]
+            k, i, j = place(g)
+            z0 = z01_t[k][:, 0, i, j : j + BLOCKS, :]
+            z1 = z01_t[k][:, 1, i, j : j + BLOCKS, :]
             outer = work.tile([P, BLOCKS, 2, R, PACK], F32, name="outer")
             for m in range(2):
                 nc.vector.tensor_tensor(
                     out=outer[:, :, m, :, :],
-                    in0=z1_t[:, :, j, :].unsqueeze(3).to_broadcast([P, BLOCKS, R, PACK]),
-                    in1=z0_t[:, :, j, m * PACK : (m + 1) * PACK]
+                    in0=z1.unsqueeze(3).to_broadcast([P, BLOCKS, R, PACK]),
+                    in1=z0[:, :, m * PACK : (m + 1) * PACK]
                     .unsqueeze(2)
                     .to_broadcast([P, BLOCKS, R, PACK]),
                     op=MULT,
@@ -134,118 +152,144 @@ def tile_fast_tucker_taylor_pa_t_kernel(tc, z, G2, out):
             krons[g] = work.tile([P, BLOCKS, 2, R, R, PACK], BF16, name="kron_t")
 
         def scalar_products(g):
-            half, j = order[g]
-            for i in range(BLOCKS):
+            k, i, j = place(g)
+            for blk in range(BLOCKS):
                 for c in range(R):
-                    if on_scalar(i, c):
+                    if on_scalar(g, blk, c):
                         nc.scalar.activation(
-                            out=krons[g][:, i, :, c, :, :],
-                            in_=outers[g][:, i, :, :, :],
+                            out=krons[g][:, blk, :, c, :, :],
+                            in_=outers[g][:, blk, :, :, :],
                             func=COPY,
-                            scale=factors[half, 2][:, i, j, c : c + 1],
+                            scale=z2_t[k][:, i, j + blk, c : c + 1],
                         )
 
-        def vector_products(g, h):
-            half, j = order[g]
-            for i in range(2 * h, 2 * h + 2):
+        def vector_products(g, blk, n):
+            k, i, j = place(g)
+            for blk in range(blk, blk + n):
                 for c in range(R):
-                    if not on_scalar(i, c):
+                    if not on_scalar(g, blk, c):
                         nc.vector.tensor_scalar(
-                            out=krons[g][:, i, :, c, :, :],
-                            in0=outers[g][:, i, :, :, :],
-                            scalar1=factors[half, 2][:, i, j, c : c + 1],
+                            out=krons[g][:, blk, :, c, :, :],
+                            in0=outers[g][:, blk, :, :, :],
+                            scalar1=z2_t[k][:, i, j + blk, c : c + 1],
                             scalar2=None,
                             op0=MULT,
                         )
 
-        def turn_half(g, h):
+        def turn(g, blk, n):
             words = krons[g][:].bitcast(F32).rearrange("p i u c b w -> p i u (c b w)")
-            bank = psum.tile([P, 2, BANK], F32, tag="turned", name="turned")
-            for i in range(2):
+            bank = psum.tile([P, 2, n * P], F32, tag="turned", name="turned")
+            for i in range(n):
                 for u in range(2):
                     nc.tensor.transpose(
-                        bank[:, u, i * P : (i + 1) * P], words[:, 2 * h + i, u, :], ident_f32[:]
+                        bank[:, u, i * P : (i + 1) * P], words[:, blk + i, u, :], ident_f32[:]
                     )
-            turned[g, h] = bank
+            turned[g, blk] = bank
 
-        def gather_half(g, h):
-            if h == 0:
+        def gather(g, blk, n):
+            if blk == 0:
                 grouped[g] = work.tile([P, GROUP, PACK], BF16, align_bytes=64, name="grouped")
             nc.scalar.copy(
-                out=grouped[g][:].bitcast(F32)[:, h * BANK : (h + 1) * BANK, :],
-                in_=turned[g, h][:].rearrange("p u n -> p n u"),
+                out=grouped[g][:].bitcast(F32)[:, blk * P : (blk + n) * P, :],
+                in_=turned[g, blk][:].rearrange("p u n -> p n u"),
             )
 
-        def quantise_and_multiply(g, first, width):
-            codes = work.tile([P, width], U32, align_bytes=64, name="codes")
-            scales = work.tile([P, width], U8, align_bytes=64, name="scales")
+        def quantise(g, blk, n):
+            codes = work.tile([P, n * P], U32, align_bytes=64, name="codes")
+            scales = work.tile([P, n * P], U8, align_bytes=64, name="scales")
             nc.vector.quantize_mx(
                 out=codes[:].bitcast(FP8X4),
                 scales=scales[:],
-                in_=grouped[g][:, first : first + width, :].rearrange("p n k -> p (n k)"),
+                in_=grouped[g][:, blk * P : (blk + n) * P, :].rearrange("p n k -> p (n k)"),
             )
+            quantised[g, blk] = codes, scales
+
+        def multiply(g, blk, t, acc):
+            codes, scales = quantised[g, blk]
+            nc.tensor.matmul_mx(
+                out=acc,
+                lhsT=g_codes[:, t * P : (t + 1) * P].bitcast(FP8X4),
+                lhsT_scale=g_scales[:, t * P : (t + 1) * P],
+                rhs=codes[:].bitcast(FP8X4),
+                rhs_scale=scales[:],
+                start=True,
+                stop=True,
+            )
+
+        def multiply_group(g):
             for t in range(Q_TILES):
-                acc = psum.tile([P, width], F32, tag="acc", name="acc")
-                nc.tensor.matmul_mx(
-                    out=acc[:],
-                    lhsT=g_codes[:, t * P : (t + 1) * P].bitcast(FP8X4),
-                    lhsT_scale=g_scales[:, t * P : (t + 1) * P],
-                    rhs=codes[:].bitcast(FP8X4),
-                    rhs_scale=scales[:],
-                    start=True,
-                    stop=True,
+                acc = psum.tile([P, 1, BLOCKS, P], F32, tag="acc", name="acc")
+                multiply(g, 0, t, acc[:, 0, :, :].rearrange("p j x -> p (j x)"))
+                accs[g, 0, t] = acc
+
+        def multiply_part(g, blk, n, tag):
+            acc = psum.tile([P, Q_TILES, n, P], F32, tag=tag, name="acc_part")
+            for t in range(Q_TILES):
+                multiply(g, blk, t, acc[:, t, :, :].rearrange("p j x -> p (j x)"))
+            accs[g, blk, 0] = acc
+
+        def leave(copy, g, blk, t):
+            acc = accs[g, blk, t]
+            tiles, n = acc.shape[1], acc.shape[2]
+            i, j = g // QUADS, g % QUADS * BLOCKS + blk
+            stage = stores.tile([P, tiles, n, P], F32, name="stage")
+            copy(
+                out=stage[:].rearrange("p t j x -> p (t j x)"),
+                in_=acc[:].rearrange("p t j x -> p (t j x)"),
+            )
+            for tile in range(tiles):
+                nc.sync.dma_start(
+                    out=out_view[:, t + tile, i, j : j + n, :], in_=stage[:, tile, :, :]
                 )
-                accs[g, first, t] = acc
 
-        def leave(g, first, width, t, on_vector=False):
-            half, j = order[g]
-            n0 = j * STRIPE + half * GROUP + first
-            stage = stores.tile([P, width], F32, name="stage")
-            if on_vector:
-                nc.vector.tensor_copy(out=stage[:], in_=accs[g, first, t][:])
-            else:
-                nc.scalar.copy(out=stage[:], in_=accs[g, first, t][:])
-            nc.sync.dma_start(out=out_view[:, t, n0 : n0 + width], in_=stage[:])
-
-        first_z = [turn_factor(0, f, "turned") for f in range(3)]
-        for f in range(3):
-            factors[0, f] = keep_factor(0, f, first_z[f])
+        keep_z(0, turn_z(0, "turned"), nc.vector.tensor_copy)
         pairs(0)
         scalar_products(0)
-        late_z = {}
-        for g in range(GROUPS):
+        keep_z(1, turn_z(1, "acc"), nc.scalar.copy)
+        vector_products(0, 0, 2)
+        turn(0, 0, 2)
+        vector_products(0, 2, 2)
+        turn(0, 2, 2)
+        pairs(1)
+        gather(0, 0, 2)
+        gather(0, 2, 2)
+        turn_g2()
+        scalar_products(1)
+        last = GROUPS - 1
+        for g in range(1, GROUPS):
+            if g >= 2:
+                quantise(g - 2, 0, BLOCKS)
+            if g < last:
+                pairs(g + 1)
             if g == 2:
                 quantise_g2()
             if g >= 2:
-                quantise_and_multiply(g - 2, 0, GROUP)
-            if g + 1 < GROUPS:
-                pairs(g + 1)
-            for h in range(2):
-                vector_products(g, h)
-                turn_half(g, h)
-            if g == 0:
-                turn_g2()
-            if g >= 1:
-                gather_half(g - 1, 0)
-                gather_half(g - 1, 1)
-            if g + 1 < GROUPS:
-                scalar_products(g + 1)
+                multiply_group(g - 2)
+            for blk in (0, 2):
+                vector_products(g, blk, 2)
+                turn(g, blk, 2)
+            if g == 8:
+                late_z = turn_z(2, "acc")
             if g >= 2:
-                leave(g - 2, 0, GROUP, 0)
-                leave(g - 2, 0, GROUP, 1)
-            if g in (8, 10, 12):
-                late_z[(g - 8) // 2] = turn_factor(1, (g - 8) // 2, "acc")
-            if g in (9, 11, 13):
-                factors[1, (g - 9) // 2] = keep_factor(1, (g - 9) // 2, late_z[(g - 9) // 2])
-        last = GROUPS - 1
-        gather_half(last, 0)
-        gather_half(last, 1)
-        quantise_and_multiply(last - 1, 0, GROUP)
-        quantise_and_multiply(last, 0, BANK)
-        leave(last - 1, 0, GROUP, 0)
-        quantise_and_multiply(last, BANK, BANK)
-        leave(last - 1, 0, GROUP, 1, True)
-        leave(last, 0, BANK, 0)
-        leave(last, 0, BANK, 1, True)
-        leave(last, BANK, BANK, 0)
-        leave(last, BANK, BANK, 1, True)
+                for blk in (0, 2):
+                    gather(g - 1, blk, 2)
+            if g < last:
+                scalar_products(g + 1)
+            if 2 <= g < last:
+                for t in range(Q_TILES):
+                    leave(nc.scalar.copy, g - 2, 0, t)
+            if g == 9:
+                keep_z(2, late_z, nc.vector.tensor_copy)
+        leave(nc.scalar.copy, last - 2, 0, 0)
+        quantise(last - 1, 0, BLOCKS)
+        multiply_group(last - 1)
+        for blk in (0, 2):
+            gather(last, blk, 2)
+        leave(nc.vector.tensor_copy, last - 2, 0, 1)
+        for blk in (0, 2):
+            quantise(last, blk, 2)
+            multiply_part(last, blk, 2, "turned")
+        for t in range(Q_TILES):
+            leave(nc.scalar.copy, last - 1, 0, t)
+        leave(nc.vector.tensor_copy, last, 0, 0)
+        leave(nc.scalar.copy, last, 2, 0)

@@ -27,6 +27,7 @@ QUADS = STRIPES // BLOCKS
 BANK = 2 * P
 GROUPS = SLICES * QUADS
 CHUNKS = ((0, 1), (1, 4), (4, 8))
+CROSSWISE = CHUNKS[1][1] * QUADS
 
 FLOPS = 2 * Q * K * B
 
@@ -99,11 +100,18 @@ def tile_fast_tucker_taylor_pa_t_kernel(tc, z, G2, out):
                 in_=turned_z[1][:].rearrange("p i x -> p (i x)"),
             )
 
-        def place(g):
-            i = g // QUADS
-            for k, (first, end) in enumerate(CHUNKS):
-                if first <= i < end:
-                    return k, i - first, g % QUADS * BLOCKS
+        def factors(g):
+            if g < CROSSWISE:
+                i, quad = divmod(g, QUADS)
+                k = 0 if i < CHUNKS[0][1] else 1
+                at = i - CHUNKS[k][0], slice(quad * BLOCKS, (quad + 1) * BLOCKS)
+            else:
+                k, at = 2, (slice(0, BLOCKS), g - CROSSWISE)
+            return (
+                z01_t[k][:, 0, at[0], at[1], :],
+                z01_t[k][:, 1, at[0], at[1], :],
+                z2_t[k][:, at[0], at[1], :],
+            )
 
         g_codes = consts.tile([P, Q], U32, align_bytes=64)
         g_scales = consts.tile([P, Q], U8, align_bytes=64)
@@ -135,9 +143,7 @@ def tile_fast_tucker_taylor_pa_t_kernel(tc, z, G2, out):
         accs = {}
 
         def pairs(g):
-            k, i, j = place(g)
-            z0 = z01_t[k][:, 0, i, j : j + BLOCKS, :]
-            z1 = z01_t[k][:, 1, i, j : j + BLOCKS, :]
+            z0, z1 = factors(g)[:2]
             outer = work.tile([P, BLOCKS, 2, R, PACK], F32, name="outer")
             for m in range(2):
                 nc.vector.tensor_tensor(
@@ -152,7 +158,7 @@ def tile_fast_tucker_taylor_pa_t_kernel(tc, z, G2, out):
             krons[g] = work.tile([P, BLOCKS, 2, R, R, PACK], BF16, name="kron_t")
 
         def scalar_products(g):
-            k, i, j = place(g)
+            z2 = factors(g)[2]
             for blk in range(BLOCKS):
                 for c in range(R):
                     if on_scalar(g, blk, c):
@@ -160,18 +166,18 @@ def tile_fast_tucker_taylor_pa_t_kernel(tc, z, G2, out):
                             out=krons[g][:, blk, :, c, :, :],
                             in_=outers[g][:, blk, :, :, :],
                             func=COPY,
-                            scale=z2_t[k][:, i, j + blk, c : c + 1],
+                            scale=z2[:, blk, c : c + 1],
                         )
 
         def vector_products(g, blk, n):
-            k, i, j = place(g)
+            z2 = factors(g)[2]
             for blk in range(blk, blk + n):
                 for c in range(R):
                     if not on_scalar(g, blk, c):
                         nc.vector.tensor_scalar(
                             out=krons[g][:, blk, :, c, :, :],
                             in0=outers[g][:, blk, :, :, :],
-                            scalar1=z2_t[k][:, i, j + blk, c : c + 1],
+                            scalar1=z2[:, blk, c : c + 1],
                             scalar2=None,
                             op0=MULT,
                         )
@@ -231,16 +237,19 @@ def tile_fast_tucker_taylor_pa_t_kernel(tc, z, G2, out):
         def leave(copy, g, blk, t):
             acc = accs[g, blk, t]
             tiles, n = acc.shape[1], acc.shape[2]
-            i, j = g // QUADS, g % QUADS * BLOCKS + blk
+            if g < CROSSWISE:
+                i, j = g // QUADS, g % QUADS * BLOCKS + blk
+                where = out_view[:, :, i, j : j + n, :]
+            else:
+                i, j = CHUNKS[2][0] + blk, g - CROSSWISE
+                where = out_view[:, :, i : i + n, j, :]
             stage = stores.tile([P, tiles, n, P], F32, name="stage")
             copy(
                 out=stage[:].rearrange("p t j x -> p (t j x)"),
                 in_=acc[:].rearrange("p t j x -> p (t j x)"),
             )
             for tile in range(tiles):
-                nc.sync.dma_start(
-                    out=out_view[:, t + tile, i, j : j + n, :], in_=stage[:, tile, :, :]
-                )
+                nc.sync.dma_start(out=where[:, t + tile, :, :], in_=stage[:, tile, :, :])
 
         keep_z(0, turn_z(0, "turned"), nc.vector.tensor_copy)
         pairs(0)

@@ -23,11 +23,11 @@ STRIPE = B // STRIPES
 SLICES = STRIPE // P
 BLOCKS = 4
 GROUP = BLOCKS * P
-QUADS = STRIPES // BLOCKS
 BANK = 2 * P
-GROUPS = SLICES * QUADS
+GROUPS = B // GROUP
 CHUNKS = ((0, 1), (1, 4), (4, 8))
-CROSSWISE = CHUNKS[1][1] * QUADS
+CROSS_QUADS = 2
+CROSSWISE = BLOCKS * CROSS_QUADS
 
 FLOPS = 2 * Q * K * B
 
@@ -49,12 +49,13 @@ def tile_fast_tucker_taylor_pa_t_kernel(tc, z, G2, out):
 
         z_view = z.rearrange("f a (j i x) -> (a j) f i x", j=STRIPES, x=P)
         z_rows = []
+        g_rows = consts.tile([P, Q_TILES, K], BF16)
         for k, (first, end) in enumerate(CHUNKS):
             rows = consts.tile([P, 3, end - first, P], BF16, name="z_rows%d" % k)
             nc.sync.dma_start(out=rows[:], in_=z_view[:, :, first:end, :])
             z_rows.append(rows)
-        g_rows = consts.tile([P, Q_TILES, K], BF16)
-        nc.scalar.dma_start(out=g_rows[:], in_=G2.rearrange("(t q) k -> q t k", q=P))
+            if k == 1:
+                nc.sync.dma_start(out=g_rows[:], in_=G2.rearrange("(t q) k -> q t k", q=P))
 
         ident_bf16 = consts.tile([P, P], BF16)
         make_identity(nc, ident_bf16[:])
@@ -84,34 +85,32 @@ def tile_fast_tucker_taylor_pa_t_kernel(tc, z, G2, out):
                     )
             return z01, z2
 
-        z01_t = {}
-        z2_t = {}
+        z01_t = consts.tile([P, 2, SLICES, STRIPES, R], BF16)
+        z2_t = consts.tile([P, SLICES, STRIPES, R], F32)
 
         def keep_z(k, turned_z, copy_z01):
-            slices = CHUNKS[k][1] - CHUNKS[k][0]
-            z01_t[k] = consts.tile([P, 2, slices, STRIPES, R], BF16, name="z01_t%d" % k)
+            first, end = CHUNKS[k]
             copy_z01(
-                out=z01_t[k][:].rearrange("p f i j a -> p (f i j a)"),
-                in_=turned_z[0][:].rearrange("p f i x -> p (f i x)"),
+                out=z01_t[:, :, first:end, :, :].rearrange("p f i j a -> p f (i j a)"),
+                in_=turned_z[0][:].rearrange("p f i x -> p f (i x)"),
             )
-            z2_t[k] = consts.tile([P, slices, STRIPES, R], F32, name="z2_t%d" % k)
             nc.scalar.copy(
-                out=z2_t[k][:].rearrange("p i j a -> p (i j a)"),
+                out=z2_t[:, first:end, :, :].rearrange("p i j a -> p (i j a)"),
                 in_=turned_z[1][:].rearrange("p i x -> p (i x)"),
             )
 
-        def factors(g):
+        def place(g, blk=0, n=BLOCKS):
             if g < CROSSWISE:
-                i, quad = divmod(g, QUADS)
-                k = 0 if i < CHUNKS[0][1] else 1
-                at = i - CHUNKS[k][0], slice(quad * BLOCKS, (quad + 1) * BLOCKS)
-            else:
-                k, at = 2, (slice(0, BLOCKS), g - CROSSWISE)
-            return (
-                z01_t[k][:, 0, at[0], at[1], :],
-                z01_t[k][:, 1, at[0], at[1], :],
-                z2_t[k][:, at[0], at[1], :],
-            )
+                i, quad = divmod(g, CROSS_QUADS)
+                j = quad * BLOCKS + blk
+                return i, slice(j, j + n)
+            half, j = divmod(g - CROSSWISE + CROSS_QUADS * BLOCKS, STRIPES)
+            i = half * BLOCKS + blk
+            return slice(i, i + n), j
+
+        def factors(g):
+            i, j = place(g)
+            return z01_t[:, 0, i, j, :], z01_t[:, 1, i, j, :], z2_t[:, i, j, :]
 
         g_codes = consts.tile([P, Q], U32, align_bytes=64)
         g_scales = consts.tile([P, Q], U8, align_bytes=64)
@@ -237,12 +236,8 @@ def tile_fast_tucker_taylor_pa_t_kernel(tc, z, G2, out):
         def leave(copy, g, blk, t):
             acc = accs[g, blk, t]
             tiles, n = acc.shape[1], acc.shape[2]
-            if g < CROSSWISE:
-                i, j = g // QUADS, g % QUADS * BLOCKS + blk
-                where = out_view[:, :, i, j : j + n, :]
-            else:
-                i, j = CHUNKS[2][0] + blk, g - CROSSWISE
-                where = out_view[:, :, i : i + n, j, :]
+            i, j = place(g, blk, n)
+            where = out_view[:, :, i, j, :]
             stage = stores.tile([P, tiles, n, P], F32, name="stage")
             copy(
                 out=stage[:].rearrange("p t j x -> p (t j x)"),

@@ -35,7 +35,7 @@ FLOPS = 2 * Q * K * B
 def on_scalar(g, blk, c):
     if g == 0:
         return c >= R - 2
-    return g < GROUPS - 8 and c == R - 1 and blk % 2 == 1
+    return g < GROUPS - 4 and c == R - 1 and blk in ((1, 2, 3) if g % 2 == 0 else (1, 3))
 
 
 def tile_fast_tucker_taylor_pa_t_kernel(tc, z, G2, out):

@@ -85,32 +85,39 @@ def tile_fast_tucker_taylor_pa_t_kernel(tc, z, G2, out):
                     )
             return z01, z2
 
-        z01_t = consts.tile([P, 2, SLICES, STRIPES, R], BF16)
-        z2_t = consts.tile([P, SLICES, STRIPES, R], F32)
+        z01_t = consts.tile([P, 2, 2, STRIPES, BLOCKS, R], BF16)
+        z2_t = consts.tile([P, 2, STRIPES, BLOCKS, R], F32)
 
         def keep_z(k, turned_z, copy_z01):
-            first, end = CHUNKS[k]
-            copy_z01(
-                out=z01_t[:, :, first:end, :, :].rearrange("p f i j a -> p f (i j a)"),
-                in_=turned_z[0][:].rearrange("p f i x -> p f (i x)"),
-            )
+            half, first = divmod(CHUNKS[k][0], BLOCKS)
+            here = slice(first, first + CHUNKS[k][1] - CHUNKS[k][0])
+            for f in range(2):
+                copy_z01(
+                    out=z01_t[:, f, half, :, here, :].rearrange("p j i a -> p i j a"),
+                    in_=turned_z[0][:, f, :, :].rearrange("p i (j a) -> p i j a", a=R),
+                )
             nc.scalar.copy(
-                out=z2_t[:, first:end, :, :].rearrange("p i j a -> p (i j a)"),
-                in_=turned_z[1][:].rearrange("p i x -> p (i x)"),
+                out=z2_t[:, half, :, here, :].rearrange("p j i a -> p i j a"),
+                in_=turned_z[1][:].rearrange("p i (j a) -> p i j a", a=R),
             )
 
         def place(g, blk=0, n=BLOCKS):
             if g < CROSSWISE:
                 i, quad = divmod(g, CROSS_QUADS)
                 j = quad * BLOCKS + blk
-                return i, slice(j, j + n)
+                return 0, i, slice(j, j + n)
             half, j = divmod(g - CROSSWISE + CROSS_QUADS * BLOCKS, STRIPES)
-            i = half * BLOCKS + blk
-            return slice(i, i + n), j
+            return half, slice(blk, blk + n), j
 
-        def factors(g):
-            i, j = place(g)
-            return z01_t[:, 0, i, j, :], z01_t[:, 1, i, j, :], z2_t[:, i, j, :]
+        def factors(g, groups=1):
+            half, i, j = place(g)
+            if g < CROSSWISE:
+                j = slice(j.start, j.start + groups * BLOCKS)
+                return z01_t[:, 0, half, j, i, :], z01_t[:, 1, half, j, i, :], z2_t[:, half, j, i, :]
+            return tuple(
+                zt[:, j : j + groups, :, :].rearrange("p j i a -> p (j i) a")
+                for zt in (z01_t[:, 0, half], z01_t[:, 1, half], z2_t[:, half])
+            )
 
         g_codes = consts.tile([P, Q], U32, align_bytes=64)
         g_scales = consts.tile([P, Q], U8, align_bytes=64)
@@ -133,7 +140,7 @@ def tile_fast_tucker_taylor_pa_t_kernel(tc, z, G2, out):
                 in_=g_grouped[:].rearrange("p t q k -> p (t q k)"),
             )
 
-        out_view = out.rearrange("(t q) (j i x) -> q t i j x", q=P, j=STRIPES, x=P)
+        out_view = out.rearrange("(t q) (j h i x) -> q t h i j x", q=P, j=STRIPES, i=BLOCKS, x=P)
         outers = {}
         krons = {}
         turned = {}
@@ -141,19 +148,23 @@ def tile_fast_tucker_taylor_pa_t_kernel(tc, z, G2, out):
         quantised = {}
         accs = {}
 
-        def pairs(g):
-            z0, z1 = factors(g)[:2]
-            outer = work.tile([P, BLOCKS, 2, R, PACK], F32, name="outer")
+        def pairs(g, groups):
+            z0, z1 = factors(g, groups)[:2]
+            blocks = groups * BLOCKS
+            outer = work.tile([P, blocks, 2, R, PACK], F32, name="outer")
             for m in range(2):
                 nc.vector.tensor_tensor(
                     out=outer[:, :, m, :, :],
-                    in0=z1.unsqueeze(3).to_broadcast([P, BLOCKS, R, PACK]),
+                    in0=z1.unsqueeze(3).to_broadcast([P, blocks, R, PACK]),
                     in1=z0[:, :, m * PACK : (m + 1) * PACK]
                     .unsqueeze(2)
-                    .to_broadcast([P, BLOCKS, R, PACK]),
+                    .to_broadcast([P, blocks, R, PACK]),
                     op=MULT,
                 )
-            outers[g] = outer
+            for n in range(groups):
+                outers[g + n] = outer[:, n * BLOCKS : (n + 1) * BLOCKS, :, :, :]
+
+        def open_group(g):
             krons[g] = work.tile([P, BLOCKS, 2, R, R, PACK], BF16, name="kron_t")
 
         def scalar_products(g):
@@ -236,8 +247,8 @@ def tile_fast_tucker_taylor_pa_t_kernel(tc, z, G2, out):
         def leave(copy, g, blk, t):
             acc = accs[g, blk, t]
             tiles, n = acc.shape[1], acc.shape[2]
-            i, j = place(g, blk, n)
-            where = out_view[:, :, i, j, :]
+            half, i, j = place(g, blk, n)
+            where = out_view[:, :, half, i, j, :]
             stage = stores.tile([P, tiles, n, P], F32, name="stage")
             copy(
                 out=stage[:].rearrange("p t j x -> p (t j x)"),
@@ -247,14 +258,16 @@ def tile_fast_tucker_taylor_pa_t_kernel(tc, z, G2, out):
                 nc.sync.dma_start(out=where[:, t + tile, :, :], in_=stage[:, tile, :, :])
 
         keep_z(0, turn_z(0, "turned"), nc.vector.tensor_copy)
-        pairs(0)
+        pairs(0, 1)
+        open_group(0)
         scalar_products(0)
         keep_z(1, turn_z(1, "acc"), nc.scalar.copy)
         vector_products(0, 0, 2)
         turn(0, 0, 2)
         vector_products(0, 2, 2)
         turn(0, 2, 2)
-        pairs(1)
+        pairs(1, 1)
+        open_group(1)
         gather(0, 0, 2)
         gather(0, 2, 2)
         turn_g2()
@@ -263,8 +276,10 @@ def tile_fast_tucker_taylor_pa_t_kernel(tc, z, G2, out):
         for g in range(1, GROUPS):
             if g >= 2:
                 quantise(g - 2, 0, BLOCKS)
+            if g < last and g % 2 == 1:
+                pairs(g + 1, 2)
             if g < last:
-                pairs(g + 1)
+                open_group(g + 1)
             if g == 2:
                 quantise_g2()
             if g >= 2:

@@ -238,11 +238,13 @@ def tile_fast_tucker_taylor_pa_t_kernel(tc, z, G2, out):
                 multiply(g, 0, t, acc[:, 0, :, :].rearrange("p j x -> p (j x)"))
                 accs[g, 0, t] = acc
 
-        def multiply_part(g, blk, n, tag):
-            acc = psum.tile([P, Q_TILES, n, P], F32, tag=tag, name="acc_part")
-            for t in range(Q_TILES):
-                multiply(g, blk, t, acc[:, t, :, :].rearrange("p j x -> p (j x)"))
-            accs[g, blk, 0] = acc
+        def multiply_part(g, blk, n, tag, banks):
+            tiles = Q_TILES // banks
+            for first in range(0, Q_TILES, tiles):
+                acc = psum.tile([P, tiles, n, P], F32, tag=tag, name="acc_part")
+                for t in range(tiles):
+                    multiply(g, blk, first + t, acc[:, t, :, :].rearrange("p j x -> p (j x)"))
+                accs[g, blk, first] = acc
 
         def leave(copy, g, blk, t):
             acc = accs[g, blk, t]
@@ -284,7 +286,7 @@ def tile_fast_tucker_taylor_pa_t_kernel(tc, z, G2, out):
                 quantise_g2()
             if g >= 2:
                 multiply_group(g - 2)
-            for blk in (0, 2):
+            for blk in (0, 2) if g < last else (0,):
                 vector_products(g, blk, 2)
                 turn(g, blk, 2)
             if g == 8:
@@ -294,21 +296,29 @@ def tile_fast_tucker_taylor_pa_t_kernel(tc, z, G2, out):
                     gather(g - 1, blk, 2)
             if g < last:
                 scalar_products(g + 1)
-            if 2 <= g < last:
+            if g >= 2:
                 for t in range(Q_TILES):
                     leave(nc.scalar.copy, g - 2, 0, t)
             if g == 9:
                 keep_z(2, late_z, nc.vector.tensor_copy)
-        leave(nc.scalar.copy, last - 2, 0, 0)
+        vector_products(last, 2, 1)
+        turn(last, 2, 1)
         quantise(last - 1, 0, BLOCKS)
         multiply_group(last - 1)
-        for blk in (0, 2):
-            gather(last, blk, 2)
-        leave(nc.vector.tensor_copy, last - 2, 0, 1)
-        for blk in (0, 2):
-            quantise(last, blk, 2)
-            multiply_part(last, blk, 2, "turned")
-        for t in range(Q_TILES):
-            leave(nc.scalar.copy, last - 1, 0, t)
-        leave(nc.vector.tensor_copy, last, 0, 0)
-        leave(nc.scalar.copy, last, 2, 0)
+        vector_products(last, 3, 1)
+        turn(last, 3, 1)
+        gather(last, 0, 2)
+        quantise(last, 0, 2)
+        leave(nc.scalar.copy, last - 1, 0, 0)
+        leave(nc.vector.tensor_copy, last - 1, 0, 1)
+        multiply_part(last, 0, 2, "turned", 1)
+        gather(last, 2, 1)
+        gather(last, 3, 1)
+        quantise(last, 2, 1)
+        multiply_part(last, 2, 1, "acc", 1)
+        quantise(last, 3, 1)
+        multiply_part(last, 3, 1, "turned", 2)
+        leave(nc.scalar.copy, last, 0, 0)
+        leave(nc.vector.tensor_copy, last, 2, 0)
+        leave(nc.vector.tensor_copy, last, 3, 0)
+        leave(nc.scalar.copy, last, 3, 1)

from contextlib import ExitStack

import concourse.mybir as mybir
from concourse.masks import make_identity

F32 = mybir.dt.float32
BF16 = mybir.dt.bfloat16
U32 = mybir.dt.uint32
U8 = mybir.dt.uint8
FP8X4 = mybir.dt.float8_e4m3fn_x4
MULT = mybir.AluOpType.mult
COPY = mybir.ActivationFunctionType.Copy

P = 128
R = 8
K = R * R * R
PACK = 4
B = 16384
Q = 256
Q_TILES = Q // P
STRIPES = P // R
STRIPE = B // STRIPES
SLICES = STRIPE // P
BLOCKS = 4
GROUP = BLOCKS * P
BANK = 2 * P
GROUPS = B // GROUP
CHUNKS = ((0, 1), (1, 4), (4, 8))
CROSS_QUADS = 2
CROSSWISE = BLOCKS * CROSS_QUADS

FLOPS = 2 * Q * K * B


def on_scalar(g, blk, c):
    if g == 0:
        return c >= R - 2
    return g < GROUPS - 4 and c == R - 1 and blk in ((1, 2, 3) if g % 2 == 0 else (1, 3))


def tile_fast_tucker_taylor_pa_t_kernel(tc, z, G2, out):
    nc = tc.nc
    with ExitStack() as ctx:
        ctx.enter_context(tc.manual_schedule())
        consts = ctx.enter_context(tc.tile_pool(name="consts", bufs=1))
        work = ctx.enter_context(tc.tile_pool(name="work", bufs=4))
        stores = ctx.enter_context(tc.tile_pool(name="stores", bufs=8))
        psum = ctx.enter_context(tc.psum_pool(name="psum", bufs=4))

        z_view = z.rearrange("f a (j i x) -> (a j) f i x", j=STRIPES, x=P)
        z_rows = []
        g_rows = consts.tile([P, Q_TILES, K], BF16)
        for k, (first, end) in enumerate(CHUNKS):
            rows = consts.tile([P, 3, end - first, P], BF16, name="z_rows%d" % k)
            nc.sync.dma_start(out=rows[:], in_=z_view[:, :, first:end, :])
            z_rows.append(rows)
            if k == 1:
                nc.sync.dma_start(out=g_rows[:], in_=G2.rearrange("(t q) k -> q t k", q=P))

        ident_bf16 = consts.tile([P, P], BF16)
        make_identity(nc, ident_bf16[:])
        ident_f32 = consts.tile([P, P], F32)
        make_identity(nc, ident_f32[:])
        by_stripe = consts.tile([P, P], BF16)
        nc.vector.tensor_copy(
            out=by_stripe[:].rearrange("p (j a) -> p j a", a=R),
            in_=ident_bf16[:].rearrange("p (a j) -> p j a", a=R),
        )
        by_stripe_z0 = consts.tile([P, P], BF16)
        nc.vector.tensor_copy(
            out=by_stripe_z0[:].rearrange("p (j m h e) -> p j m h e", m=2, h=2, e=2),
            in_=ident_bf16[:].rearrange("p (h m e j) -> p j m h e", m=2, h=2, e=2),
        )

        def turn_z(k, tag):
            slices = CHUNKS[k][1] - CHUNKS[k][0]
            z01 = psum.tile([P, 2, slices, P], BF16, tag=tag, name="z01")
            z2 = psum.tile([P, slices, P], BF16, tag=tag, name="z2")
            for f in range(3):
                for i in range(slices):
                    nc.tensor.transpose(
                        z2[:, i, :] if f == 2 else z01[:, f, i, :],
                        z_rows[k][:, f, i, :],
                        by_stripe_z0[:] if f == 0 else by_stripe[:],
                    )
            return z01, z2

        z01_t = consts.tile([P, 2, 2, STRIPES, BLOCKS, R], BF16)
        z2_t = consts.tile([P, 2, STRIPES, BLOCKS, R], F32)

        def keep_z(k, turned_z, copy_z01):
            half, first = divmod(CHUNKS[k][0], BLOCKS)
            here = slice(first, first + CHUNKS[k][1] - CHUNKS[k][0])
            for f in range(2):
                copy_z01(
                    out=z01_t[:, f, half, :, here, :].rearrange("p j i a -> p i j a"),
                    in_=turned_z[0][:, f, :, :].rearrange("p i (j a) -> p i j a", a=R),
                )
            nc.scalar.copy(
                out=z2_t[:, half, :, here, :].rearrange("p j i a -> p i j a"),
                in_=turned_z[1][:].rearrange("p i (j a) -> p i j a", a=R),
            )

        def place(g, blk=0, n=BLOCKS):
            if g < CROSSWISE:
                i, quad = divmod(g, CROSS_QUADS)
                j = quad * BLOCKS + blk
                return 0, i, slice(j, j + n)
            half, j = divmod(g - CROSSWISE + CROSS_QUADS * BLOCKS, STRIPES)
            return half, slice(blk, blk + n), j

        def factors(g, groups=1):
            half, i, j = place(g)
            if g < CROSSWISE:
                j = slice(j.start, j.start + groups * BLOCKS)
                return z01_t[:, 0, half, j, i, :], z01_t[:, 1, half, j, i, :], z2_t[:, half, j, i, :]
            return tuple(
                zt[:, j : j + groups, :, :].rearrange("p j i a -> p (j i) a")
                for zt in (z01_t[:, 0, half], z01_t[:, 1, half], z2_t[:, half])
            )

        g_codes = consts.tile([P, Q], U32, align_bytes=64)
        g_scales = consts.tile([P, Q], U8, align_bytes=64)
        g_grouped = consts.tile([P, Q_TILES, P, PACK], BF16, align_bytes=64)

        def turn_g2():
            g_words = g_rows[:].bitcast(F32).rearrange("q t (p u) -> q t u p", u=2)
            g_turned = psum.tile([P, Q_TILES, 2, P], F32, tag="acc")
            for t in range(Q_TILES):
                for u in range(2):
                    nc.tensor.transpose(g_turned[:, t, u, :], g_words[:, t, u, :], ident_f32[:])
            nc.scalar.copy(
                out=g_grouped[:].bitcast(F32), in_=g_turned[:].rearrange("p t u q -> p t q u")
            )

        def quantise_g2():
            nc.vector.quantize_mx(
                out=g_codes[:].bitcast(FP8X4),
                scales=g_scales[:],
                in_=g_grouped[:].rearrange("p t q k -> p (t q k)"),
            )

        out_view = out.rearrange("(t q) (j h i x) -> q t h i j x", q=P, j=STRIPES, i=BLOCKS, x=P)
        outers = {}
        krons = {}
        turned = {}
        grouped = {}
        quantised = {}
        accs = {}

        def pairs(g, groups):
            z0, z1 = factors(g, groups)[:2]
            blocks = groups * BLOCKS
            outer = work.tile([P, blocks, 2, R, PACK], F32, name="outer")
            for m in range(2):
                nc.vector.tensor_tensor(
                    out=outer[:, :, m, :, :],
                    in0=z1.unsqueeze(3).to_broadcast([P, blocks, R, PACK]),
                    in1=z0[:, :, m * PACK : (m + 1) * PACK]
                    .unsqueeze(2)
                    .to_broadcast([P, blocks, R, PACK]),
                    op=MULT,
                )
            for n in range(groups):
                outers[g + n] = outer[:, n * BLOCKS : (n + 1) * BLOCKS, :, :, :]

        def open_group(g):
            krons[g] = work.tile([P, BLOCKS, 2, R, R, PACK], BF16, name="kron_t")

        def scalar_products(g):
            z2 = factors(g)[2]
            for blk in range(BLOCKS):
                for c in range(R):
                    if on_scalar(g, blk, c):
                        nc.scalar.activation(
                            out=krons[g][:, blk, :, c, :, :],
                            in_=outers[g][:, blk, :, :, :],
                            func=COPY,
                            scale=z2[:, blk, c : c + 1],
                        )

        def vector_products(g, blk, n):
            z2 = factors(g)[2]
            for blk in range(blk, blk + n):
                for c in range(R):
                    if not on_scalar(g, blk, c):
                        nc.vector.tensor_scalar(
                            out=krons[g][:, blk, :, c, :, :],
                            in0=outers[g][:, blk, :, :, :],
                            scalar1=z2[:, blk, c : c + 1],
                            scalar2=None,
                            op0=MULT,
                        )

        def turn(g, blk, n):
            words = krons[g][:].bitcast(F32).rearrange("p i u c b w -> p i u (c b w)")
            bank = psum.tile([P, 2, n * P], F32, tag="turned", name="turned")
            for i in range(n):
                for u in range(2):
                    nc.tensor.transpose(
                        bank[:, u, i * P : (i + 1) * P], words[:, blk + i, u, :], ident_f32[:]
                    )
            turned[g, blk] = bank

        def gather(g, blk, n):
            if blk == 0:
                grouped[g] = work.tile([P, GROUP, PACK], BF16, align_bytes=64, name="grouped")
            nc.scalar.copy(
                out=grouped[g][:].bitcast(F32)[:, blk * P : (blk + n) * P, :],
                in_=turned[g, blk][:].rearrange("p u n -> p n u"),
            )

        def quantise(g, blk, n):
            codes = work.tile([P, n * P], U32, align_bytes=64, name="codes")
            scales = work.tile([P, n * P], U8, align_bytes=64, name="scales")
            nc.vector.quantize_mx(
                out=codes[:].bitcast(FP8X4),
                scales=scales[:],
                in_=grouped[g][:, blk * P : (blk + n) * P, :].rearrange("p n k -> p (n k)"),
            )
            quantised[g, blk] = codes, scales

        def multiply(g, blk, t, acc):
            codes, scales = quantised[g, blk]
            nc.tensor.matmul_mx(
                out=acc,
                lhsT=g_codes[:, t * P : (t + 1) * P].bitcast(FP8X4),
                lhsT_scale=g_scales[:, t * P : (t + 1) * P],
                rhs=codes[:].bitcast(FP8X4),
                rhs_scale=scales[:],
                start=True,
                stop=True,
            )

        def multiply_group(g):
            for t in range(Q_TILES):
                acc = psum.tile([P, 1, BLOCKS, P], F32, tag="acc", name="acc")
                multiply(g, 0, t, acc[:, 0, :, :].rearrange("p j x -> p (j x)"))
                accs[g, 0, t] = acc

        def multiply_part(g, blk, n, tag, banks):
            tiles = Q_TILES // banks
            for first in range(0, Q_TILES, tiles):
                acc = psum.tile([P, tiles, n, P], F32, tag=tag, name="acc_part")
                for t in range(tiles):
                    multiply(g, blk, first + t, acc[:, t, :, :].rearrange("p j x -> p (j x)"))
                accs[g, blk, first] = acc

        def leave(copy, g, blk, t):
            acc = accs[g, blk, t]
            tiles, n = acc.shape[1], acc.shape[2]
            half, i, j = place(g, blk, n)
            where = out_view[:, :, half, i, j, :]
            stage = stores.tile([P, tiles, n, P], F32, name="stage")
            copy(
                out=stage[:].rearrange("p t j x -> p (t j x)"),
                in_=acc[:].rearrange("p t j x -> p (t j x)"),
            )
            for tile in range(tiles):
                nc.sync.dma_start(out=where[:, t + tile, :, :], in_=stage[:, tile, :, :])

        keep_z(0, turn_z(0, "turned"), nc.vector.tensor_copy)
        pairs(0, 1)
        open_group(0)
        scalar_products(0)
        keep_z(1, turn_z(1, "acc"), nc.scalar.copy)
        vector_products(0, 0, 2)
        turn(0, 0, 2)
        vector_products(0, 2, 2)
        turn(0, 2, 2)
        pairs(1, 1)
        open_group(1)
        gather(0, 0, 2)
        gather(0, 2, 2)
        turn_g2()
        scalar_products(1)
        last = GROUPS - 1
        for g in range(1, GROUPS):
            if g >= 2:
                quantise(g - 2, 0, BLOCKS)
            if g < last and g % 2 == 1:
                pairs(g + 1, 2)
            if g < last:
                open_group(g + 1)
            if g == 2:
                quantise_g2()
            if g >= 2:
                multiply_group(g - 2)
            for blk in (0, 2) if g < last else (0,):
                vector_products(g, blk, 2)
                turn(g, blk, 2)
            if g == 8:
                late_z = turn_z(2, "acc")
            if g >= 2:
                for blk in (0, 2):
                    gather(g - 1, blk, 2)
            if g < last:
                scalar_products(g + 1)
            if g >= 2:
                for t in range(Q_TILES):
                    leave(nc.scalar.copy, g - 2, 0, t)
            if g == 9:
                keep_z(2, late_z, nc.vector.tensor_copy)
        vector_products(last, 2, 1)
        turn(last, 2, 1)
        quantise(last - 1, 0, BLOCKS)
        multiply_group(last - 1)
        vector_products(last, 3, 1)
        turn(last, 3, 1)
        gather(last, 0, 2)
        quantise(last, 0, 2)
        leave(nc.scalar.copy, last - 1, 0, 0)
        leave(nc.vector.tensor_copy, last - 1, 0, 1)
        multiply_part(last, 0, 2, "turned", 1)
        gather(last, 2, 1)
        gather(last, 3, 1)
        quantise(last, 2, 1)
        multiply_part(last, 2, 1, "acc", 1)
        quantise(last, 3, 1)
        multiply_part(last, 3, 1, "turned", 2)
        leave(nc.scalar.copy, last, 0, 0)
        leave(nc.vector.tensor_copy, last, 2, 0)
        leave(nc.vector.tensor_copy, last, 3, 0)
        leave(nc.scalar.copy, last, 3, 1)
